import numpy as np
import ml_dtypes


def mxq(x, axis, fmt="e4m3"):
    dtype, down = {"e4m3": (ml_dtypes.float8_e4m3fn, 7), "e5m2": (ml_dtypes.float8_e5m2, 14)}[fmt]
    v = np.moveaxis(np.asarray(x, np.float32).astype(ml_dtypes.bfloat16).astype(np.float64), axis, -1)
    blocks = v.reshape(v.shape[:-1] + (-1, 32))
    amax = np.abs(blocks).max(-1, keepdims=True)
    byte = np.maximum(np.where(amax > 0, np.frexp(amax)[1] - 1 + 127, 0) - down, 1)
    scale = np.exp2(byte - 127.0)
    codes = (blocks / scale).astype(np.float32).astype(dtype).astype(np.float64)
    return np.moveaxis((codes * scale).reshape(v.shape), -1, axis)


WIDE = False


def mx_kscale(k):
    if not WIDE:
        return np.ones(k)
    levels = np.array([10, -10, 5, -5, 0])
    a = np.random.permutation(np.resize(levels, k // 512 * 4)).reshape(k // 512, 4)
    idx = np.arange(k)
    return np.exp2(a[idx // 512, idx % 128 // 32])


BF16 = ml_dtypes.bfloat16


def bf(x):
    return np.asarray(x, np.float32).astype(BF16)


def f64(x):
    return np.asarray(x).astype(np.float64)


B, D, H, NH, P, KC = 256, 2048, 2048, 4, 2560, 4
DI = D // NH
DH = H // NH


def silu(v):
    return v / (1.0 + np.exp(-v))


def sigmoid(v):
    return 1.0 / (1.0 + np.exp(-v))


def layer_norm(v, g, b):
    mu = v.mean(-1, keepdims=True)
    var = ((v - mu) ** 2).mean(-1, keepdims=True)
    return (v - mu) / np.sqrt(var + 1e-5) * g + b


def heads(v):
    return v.reshape(v.shape[0], NH, -1).transpose(1, 0, 2)


def block_linear(vq, w, b):
    y = vq @ mxq(f64(w), 1, "e4m3")
    return y.transpose(1, 0, 2).reshape(y.shape[1], H) + f64(b)


def setup_inputs():
    rn = np.random.standard_normal
    s = mx_kscale(DH)
    sw, sr = 0.7 / np.sqrt(DI), 0.7 / np.sqrt(DH)
    inp = {
        "x": bf(rn((B, D)) * (0.7 + 0.6 * np.random.random((B, 1))) + 0.3 * rn((B, 1))),
        "h_prev": bf(rn((B, H)) * np.tile(s, NH)),
        "c_prev": bf(rn((B, H))),
        "n_prev": bf(0.5 + np.random.random((B, H))),
        "m_prev": bf(rn((B, H)) * 0.5),
        "ln_g": bf(1.0 + 0.1 * rn(D)),
        "ln_b": bf(0.3 * rn(D)),
        "conv_w": bf((0.35 + 0.3 * np.random.random(KC)) * np.sign(rn(KC))),
        "conv_b": bf(0.3 + 0.05 * rn(1)),
    }
    for nm in ("wz", "wi", "wf", "wo"):
        inp[nm + "_w"] = bf(rn((NH, DI, DH)) * sw)
        inp[nm + "_b"] = bf(rn(H) * 0.2)
    for nm in ("rz", "ri", "rf", "ro"):
        inp[nm + "_w"] = bf(rn((NH, DH, DH)) * sr / s[None, :, None])
        inp[nm + "_b"] = bf(rn(H) * 0.2)
    return inp


def reference(x, h_prev, c_prev, n_prev, m_prev, ln_g, ln_b, conv_w, conv_b,
              wz_w, wz_b, wi_w, wi_b, wf_w, wf_b, wo_w, wo_b,
              rz_w, rz_b, ri_w, ri_b, rf_w, rf_b, ro_w, ro_b):
    x, cw = f64(x), f64(conv_w)
    x_norm = layer_norm(x, f64(ln_g), f64(ln_b))
    xp = np.pad(x_norm, ((0, 0), (KC - 1, 0)))
    xc = f64(conv_b) + sum(cw[k] * xp[:, k:k + D] for k in range(KC))
    x_conv = silu(xc)

    xq = mxq(heads(x), 2, "e4m3")
    cq = mxq(heads(x_conv), 2, "e4m3")
    hq = mxq(heads(f64(h_prev)), 2, "e4m3")

    z = np.tanh(block_linear(xq, wz_w, wz_b) + block_linear(hq, rz_w, rz_b))
    o = sigmoid(block_linear(xq, wo_w, wo_b) + block_linear(hq, ro_w, ro_b))
    i_tilde = block_linear(cq, wi_w, wi_b) + block_linear(hq, ri_w, ri_b)
    f_tilde = block_linear(cq, wf_w, wf_b) + block_linear(hq, rf_w, rf_b)

    m_t = np.maximum(f_tilde + f64(m_prev), i_tilde)
    i_g = np.exp(i_tilde - m_t)
    f_g = np.exp(f_tilde + f64(m_prev) - m_t)
    c_t = f_g * f64(c_prev) + i_g * z
    n_t = f_g * f64(n_prev) + i_g
    h_t = o * c_t / (n_t + 1e-6)
    return (h_t, c_t, n_t, m_t)

@@ -1,0 +1,359 @@
+from contextlib import ExitStack
+
+import concourse.mybir as mybir
+from concourse.masks import make_identity
+
+F32 = mybir.dt.float32
+BF16 = mybir.dt.bfloat16
+U32 = mybir.dt.uint32
+U8 = mybir.dt.uint8
+FP8X4 = mybir.dt.float8_e4m3fn_x4
+ACT = mybir.ActivationFunctionType
+ALU = mybir.AluOpType
+
+P = 128
+B = 256
+BT = B // P
+D = 2048
+NH = 4
+DH = D // NH
+PACK = 4
+NT = D // P
+TPH = DH // P
+KC = 4
+LN_EPS = 1e-5
+H_EPS = 1e-6
+GZ, GI, GF, GO = 0, 1, 2, 3
+
+FLOPS = 8 * 2 * B * D * DH
+
+
+def batch_tiles(ap):
+    return ap.rearrange("(t p) d -> p t d", p=P)
+
+
+def tile_slstmblock_pa_kernel(
+    tc,
+    x, h_prev, c_prev, n_prev, m_prev, ln_g, ln_b, conv_w, conv_b,
+    wz_w, wz_b, wi_w, wi_b, wf_w, wf_b, wo_w, wo_b,
+    rz_w, rz_b, ri_w, ri_b, rf_w, rf_b, ro_w, ro_b,
+    out_h, out_c, out_n, out_m,
+):
+    nc = tc.nc
+    in_weights = (wz_w, wi_w, wf_w, wo_w)
+    rec_weights = (rz_w, ri_w, rf_w, ro_w)
+
+    with ExitStack() as stack:
+        keep = stack.enter_context(tc.tile_pool(name="keep", bufs=1))
+        w_raw_pool = stack.enter_context(tc.tile_pool(name="w_raw", bufs=6))
+        w_grp_pool = stack.enter_context(tc.tile_pool(name="w_grp", bufs=4))
+        w_mx_pool = stack.enter_context(tc.tile_pool(name="w_mx", bufs=2))
+
+        ident_f32 = keep.tile([P, P], F32)
+        make_identity(nc, ident_f32[:])
+        ident_bf = keep.tile([P, P], BF16)
+        make_identity(nc, ident_bf[:])
+        minus_half = keep.tile([P, 1], F32)
+        nc.vector.memset(minus_half[:], -0.5)
+        two_eps = keep.tile([P, 1], F32)
+        nc.vector.memset(two_eps[:], 2.0 * H_EPS)
+
+        act_codes = {}
+        act_scales = {}
+        for name in ("x", "h", "c"):
+            act_codes[name] = keep.tile([P, NH, B], U32, name="codes_" + name, align_bytes=64)
+            act_scales[name] = keep.tile([P, NH, B], U8, name="scales_" + name, align_bytes=64)
+
+        m_prev_t = keep.tile([P, NT, B], BF16)
+        cn_prev = keep.tile([P, 2, BT, D], BF16)
+        gate_bias = keep.tile([P, 4, NT], F32)
+        half_o_bias = keep.tile([P, NT], F32)
+
+        def quantise_weight(w_head, pair_order, slot, on_vector):
+            raw = w_raw_pool.tile([P, PACK, DH], BF16)
+            if pair_order:
+                nc.sync.dma_start(
+                    out=raw[:].rearrange("q (u e) n -> q u (e n)", u=2),
+                    in_=w_head.rearrange("(u q e) n -> q u (e n)", u=2, e=2),
+                )
+            else:
+                nc.sync.dma_start(out=raw[:], in_=w_head.rearrange("(t p) n -> p t n", p=P))
+            grouped = w_grp_pool.tile([P, DH, PACK], BF16, align_bytes=64)
+            dst = grouped[:].rearrange("p (c i) t -> p c t i", i=4)
+            src = raw[:].rearrange("p t (c i) -> p c t i", i=4)
+            if on_vector:
+                nc.vector.tensor_copy(out=dst, in_=src)
+            else:
+                nc.scalar.copy(out=dst, in_=src)
+            codes = w_mx_pool.tile([P, DH], U32, tag="codes%d" % slot, align_bytes=64)
+            scales = w_mx_pool.tile([P, DH], U8, tag="scales%d" % slot, align_bytes=64)
+            nc.vector.quantize_mx(
+                out=codes[:].bitcast(FP8X4),
+                scales=scales[:],
+                in_=grouped[:].rearrange("p n t -> p (n t)"),
+            )
+            return codes, scales
+
+        weight_list = []
+        for gate in (GZ, GO, GI, GF):
+            weight_list.append(("in", gate))
+            weight_list.append(("rec", gate))
+        head_weights = [{} for head in range(NH)]
+
+        def quantise_head_weight(head, slot):
+            kind, gate = weight_list[slot]
+            w = in_weights[gate] if kind == "in" else rec_weights[gate]
+            pair_order = not (kind == "in" and gate in (GI, GF))
+            head_weights[head][(kind, gate)] = quantise_weight(w[head], pair_order, slot, slot % 2 == 0)
+
+        with tc.tile_pool(name="pro", bufs=1) as pro, tc.psum_pool(name="pro_psum", bufs=2) as pro_psum:
+            x_sb = pro.tile([P, BT, D], BF16)
+            h_sb = pro.tile([P, BT, D], BF16)
+            m_sb = pro.tile([P, BT, D], BF16)
+            for t in range(BT):
+                nc.sync.dma_start(out=x_sb[:, t, :], in_=x[t * P:(t + 1) * P, :])
+            nc.sync.dma_start(out=h_sb[:], in_=batch_tiles(h_prev))
+            nc.sync.dma_start(out=m_sb[:], in_=batch_tiles(m_prev))
+
+            bias_rows = pro.tile([P, P], BF16)
+            ln_rows = pro.tile([P, P], BF16)
+            nc.vector.memset(ln_rows[:], 0.0)
+            taps_bf = pro.tile([P, KC], BF16)
+            conv_bias_bf = pro.tile([P, 1], BF16)
+            with nc.allow_non_contiguous_dma(reason="small vectors"):
+                for v, vec in enumerate((ln_g, ln_b)):
+                    nc.gpsimd.dma_start(out=ln_rows[NT * v:NT * (v + 1), :], in_=vec.rearrange("(r c) -> r c", c=P))
+                nc.gpsimd.dma_start(out=taps_bf[:], in_=conv_w.partition_broadcast(P))
+                nc.gpsimd.dma_start(out=conv_bias_bf[:], in_=conv_b.partition_broadcast(P))
+                for v, vec in enumerate((wz_b, wi_b, wf_b, wo_b, rz_b, ri_b, rf_b, ro_b)):
+                    nc.gpsimd.dma_start(out=bias_rows[NT * v:NT * (v + 1), :], in_=vec.rearrange("(r c) -> r c", c=P))
+
+            taps = pro.tile([P, KC], F32)
+            nc.vector.tensor_copy(out=taps[:], in_=taps_bf[:])
+            conv_bias = pro.tile([P, 1], F32)
+            nc.vector.tensor_copy(out=conv_bias[:], in_=conv_bias_bf[:])
+
+            band = pro.tile([P, 2 * P], F32)
+            nc.vector.memset(band[:], 0.0)
+            for s in range(KC):
+                nc.vector.scalar_tensor_tensor(
+                    out=band[:, s:s + P], in0=ident_f32[:], scalar=taps[:, KC - 1 - s:KC - s],
+                    in1=band[:, s:s + P], op0=ALU.mult, op1=ALU.add,
+                )
+
+            vec_t = pro_psum.tile([P, 2, P], BF16, bufs=1)
+            nc.tensor.transpose(out=vec_t[:, 0, :], in_=bias_rows[:], identity=ident_bf[:])
+            nc.tensor.transpose(out=vec_t[:, 1, :], in_=ln_rows[:], identity=ident_bf[:])
+            vec_cols = pro.tile([P, 2, P], F32)
+            nc.vector.tensor_copy(out=vec_cols[:], in_=vec_t[:])
+            nc.vector.tensor_tensor(
+                out=gate_bias[:].rearrange("p g r -> p (g r)"),
+                in0=vec_cols[:, 0, 0:4 * NT], in1=vec_cols[:, 0, 4 * NT:8 * NT], op=ALU.add,
+            )
+            nc.vector.tensor_scalar_mul(out=half_o_bias[:], in0=gate_bias[:, GO, :], scalar1=0.5)
+
+            stats = pro.tile([P, BT, NH, 6], F32)
+            mean_var = pro.tile([P, BT, 2], F32)
+            var_eps = pro.tile([P, BT], F32)
+            rstd = pro.tile([P, BT], F32)
+            shift = pro.tile([P, BT], F32)
+            for t in range(BT):
+                for head in range(NH):
+                    nc.vector.bn_stats(out=stats[:, t, head, :], in_=x_sb[:, t, head * DH:(head + 1) * DH])
+                nc.vector.bn_aggr(out=mean_var[:, t, :], in_=stats[:, t, :, :].rearrange("p c s -> p (c s)"))
+                nc.vector.tensor_scalar_add(out=var_eps[:, t:t + 1], in0=mean_var[:, t, 1:2], scalar1=LN_EPS)
+                nc.gpsimd.tensor_tensor(out=rstd[:, t:t + 1], in0=var_eps[:, t:t + 1], in1=minus_half[:], op=ALU.pow)
+                nc.vector.scalar_tensor_tensor(
+                    out=shift[:, t:t + 1], in0=mean_var[:, t, 0:1], scalar=-1.0, in1=rstd[:, t:t + 1],
+                    op0=ALU.mult, op1=ALU.mult,
+                )
+            x_hat = pro.tile([P, BT, D], F32)
+            for head in range(NH):
+                for t in range(BT):
+                    cols = slice(head * DH, (head + 1) * DH)
+                    nc.scalar.activation(
+                        out=x_hat[:, t, cols], in_=x_sb[:, t, cols], func=ACT.Identity,
+                        scale=rstd[:, t:t + 1], bias=shift[:, t:t + 1],
+                    )
+
+            def transpose_pairs(src, name):
+                grouped = pro.tile([P, NH, B, PACK], BF16, name="grp_" + name, align_bytes=64)
+                for head in range(NH):
+                    words_t = pro_psum.tile([P, 2, B], F32, tag="words_t")
+                    for u in range(2):
+                        for t in range(BT):
+                            first = head * (DH // 2) + u * P
+                            nc.tensor.transpose(
+                                out=words_t[:, u, t * P:(t + 1) * P],
+                                in_=src[:, t, :].bitcast(F32)[:, first:first + P],
+                                identity=ident_f32[:],
+                            )
+                    nc.scalar.copy(
+                        out=grouped[:, head, :, :].bitcast(F32),
+                        in_=words_t[:].rearrange("p u b -> p b u"),
+                    )
+                    nc.vector.quantize_mx(
+                        out=act_codes[name][:, head, :].bitcast(FP8X4),
+                        scales=act_scales[name][:, head, :],
+                        in_=grouped[:, head, :, :].rearrange("p b t -> p (b t)"),
+                    )
+
+            transpose_pairs(x_sb, "x")
+
+            x_norm_t = pro.tile([P, NT, B], F32)
+            for pair in range(NT // 2):
+                x_hat_t = pro_psum.tile([P, 2, B], F32, tag="x_hat_t")
+                for i in range(2):
+                    r = 2 * pair + i
+                    for t in range(BT):
+                        nc.tensor.transpose(
+                            out=x_hat_t[:, i, t * P:(t + 1) * P], in_=x_hat[:, t, r * P:(r + 1) * P],
+                            identity=ident_f32[:],
+                        )
+                for i in range(2):
+                    r = 2 * pair + i
+                    nc.vector.tensor_scalar(
+                        out=x_norm_t[:, r, :], in0=x_hat_t[:, i, :],
+                        scalar1=vec_cols[:, 1, r:r + 1], scalar2=vec_cols[:, 1, NT + r:NT + r + 1],
+                        op0=ALU.mult, op1=ALU.add,
+                    )
+
+            c_grouped = pro.tile([P, NH, B, PACK], BF16, align_bytes=64)
+            for head in range(NH):
+                for t in range(BT):
+                    rows = slice(t * P, (t + 1) * P)
+                    conv_t = pro_psum.tile([P, TPH, P], F32, tag="conv_t")
+                    for j in range(TPH):
+                        r = head * TPH + j
+                        nc.tensor.matmul(
+                            out=conv_t[:, j, :], lhsT=band[:, 0:P], rhs=x_norm_t[:, r, rows],
+                            start=True, stop=(r == 0),
+                        )
+                        if r > 0:
+                            nc.tensor.matmul(
+                                out=conv_t[:, j, :], lhsT=band[:, P:2 * P], rhs=x_norm_t[:, r - 1, rows],
+                                start=False, stop=True,
+                            )
+                    nc.scalar.activation(
+                        out=c_grouped[:, head, rows, :], in_=conv_t[:].rearrange("p j b -> p b j"),
+                        func=ACT.Silu, bias=conv_bias[:, 0:1],
+                    )
+                nc.vector.quantize_mx(
+                    out=act_codes["c"][:, head, :].bitcast(FP8X4),
+                    scales=act_scales["c"][:, head, :],
+                    in_=c_grouped[:, head, :, :].rearrange("p b t -> p (b t)"),
+                )
+
+            transpose_pairs(h_sb, "h")
+
+            for head in range(NH):
+                m_prev_ps = pro_psum.tile([P, TPH, B], BF16, bufs=1)
+                for j in range(TPH):
+                    r = head * TPH + j
+                    for t in range(BT):
+                        nc.tensor.transpose(
+                            out=m_prev_ps[:, j, t * P:(t + 1) * P], in_=m_sb[:, t, r * P:(r + 1) * P],
+                            identity=ident_bf[:],
+                        )
+                nc.scalar.copy(out=m_prev_t[:, head * TPH:(head + 1) * TPH, :], in_=m_prev_ps[:])
+
+        for slot in range(len(weight_list)):
+            quantise_head_weight(0, slot)
+        nc.sync.dma_start(out=cn_prev[:, 0, :, :], in_=batch_tiles(c_prev))
+        nc.sync.dma_start(out=cn_prev[:, 1, :, :], in_=batch_tiles(n_prev))
+
+        work = stack.enter_context(tc.tile_pool(name="work", bufs=2))
+        stage = stack.enter_context(tc.tile_pool(name="stage", bufs=2))
+        gate_psum = stack.enter_context(tc.psum_pool(name="gate_psum", bufs=2))
+        back_psum = stack.enter_context(tc.psum_pool(name="back_psum", bufs=1))
+
+        def gate_matmuls(out, head, gate, in_name, cols):
+            for kind, name, first in (("in", in_name, True), ("rec", "h", False)):
+                codes, scales = head_weights[head][(kind, gate)]
+                nc.tensor.matmul_mx(
+                    out=out,
+                    lhsT=codes[:, cols].bitcast(FP8X4), lhsT_scale=scales[:, cols],
+                    rhs=act_codes[name][:, head, :].bitcast(FP8X4), rhs_scale=act_scales[name][:, head, :],
+                    start=first, stop=not first,
+                )
+
+        for head in range(NH):
+            cn_new = stage.tile([P, 2, BT, DH], F32)
+            oc_new = stage.tile([P, BT, DH], F32)
+            m_new = stage.tile([P, BT, DH], F32)
+            for j in range(TPH):
+                r = head * TPH + j
+                cols = slice(j * P, (j + 1) * P)
+                zo = gate_psum.tile([P, 2, B], F32)
+                gate_matmuls(zo[:, 0, :], head, GZ, "x", cols)
+                gate_matmuls(zo[:, 1, :], head, GO, "x", cols)
+                i_f = gate_psum.tile([P, 2, B], F32)
+                gate_matmuls(i_f[:, 0, :], head, GI, "c", cols)
+                gate_matmuls(i_f[:, 1, :], head, GF, "c", cols)
+
+                z = work.tile([P, B], F32)
+                nc.scalar.activation(out=z[:], in_=zo[:, 0, :], func=ACT.Tanh, bias=gate_bias[:, GZ, r:r + 1])
+                tanh_o = work.tile([P, B], F32)
+                nc.scalar.activation(
+                    out=tanh_o[:], in_=zo[:, 1, :], func=ACT.Tanh, bias=half_o_bias[:, r:r + 1], scale=0.5,
+                )
+                f_m = work.tile([P, B], F32)
+                nc.vector.scalar_tensor_tensor(
+                    out=f_m[:], in0=i_f[:, 1, :], scalar=gate_bias[:, GF, r:r + 1], in1=m_prev_t[:, r, :],
+                    op0=ALU.add, op1=ALU.add,
+                )
+                m_t = work.tile([P, B], F32)
+                nc.vector.scalar_tensor_tensor(
+                    out=m_t[:], in0=i_f[:, 0, :], scalar=gate_bias[:, GI, r:r + 1], in1=f_m[:],
+                    op0=ALU.add, op1=ALU.max,
+                )
+                below = work.tile([P, 2, B], F32)
+                nc.vector.scalar_tensor_tensor(
+                    out=below[:, 0, :], in0=i_f[:, 0, :], scalar=gate_bias[:, GI, r:r + 1], in1=m_t[:],
+                    op0=ALU.add, op1=ALU.subtract,
+                )
+                nc.vector.tensor_tensor(out=below[:, 1, :], in0=f_m[:], in1=m_t[:], op=ALU.subtract)
+                ig_fg = work.tile([P, 2, B], F32)
+                nc.scalar.activation(out=ig_fg[:], in_=below[:], func=ACT.Exp)
+                ig_z = work.tile([P, B], F32)
+                nc.vector.tensor_tensor(out=ig_z[:], in0=ig_fg[:, 0, :], in1=z[:], op=ALU.mult)
+
+                back_add = back_psum.tile([P, 2, BT, P], F32)
+                back_mul = back_psum.tile([P, 2, BT, P], F32)
+                back_m = back_psum.tile([P, BT, P], F32)
+                for t in range(BT):
+                    rows = slice(t * P, (t + 1) * P)
+                    nc.tensor.transpose(out=back_mul[:, 0, t, :], in_=ig_fg[:, 1, rows], identity=ident_f32[:])
+                    nc.tensor.transpose(out=back_add[:, 0, t, :], in_=ig_z[:, rows], identity=ident_f32[:])
+                    nc.tensor.transpose(out=back_add[:, 1, t, :], in_=ig_fg[:, 0, rows], identity=ident_f32[:])
+                    nc.tensor.transpose(out=back_mul[:, 1, t, :], in_=tanh_o[:, rows], identity=ident_f32[:])
+                    nc.tensor.transpose(out=back_m[:, t, :], in_=m_t[:, rows], identity=ident_f32[:])
+
+                kept = work.tile([P, 2, BT, P], F32)
+                nc.vector.tensor_tensor(
+                    out=kept[:], in0=cn_prev[:, :, :, r * P:(r + 1) * P],
+                    in1=back_mul[:, 0:1, :, :].to_broadcast([P, 2, BT, P]), op=ALU.mult,
+                )
+                nc.vector.tensor_tensor(out=cn_new[:, :, :, cols], in0=kept[:], in1=back_add[:], op=ALU.add)
+                nc.vector.scalar_tensor_tensor(
+                    out=oc_new[:, :, cols], in0=back_mul[:, 1, :, :], scalar=1.0, in1=cn_new[:, 0, :, cols],
+                    op0=ALU.add, op1=ALU.mult,
+                )
+                nc.scalar.copy(out=m_new[:, :, cols], in_=back_m[:])
+
+                if head + 1 < NH:
+                    quantise_head_weight(head + 1, 2 * j)
+                    quantise_head_weight(head + 1, 2 * j + 1)
+
+            log_den = stage.tile([P, BT, DH], F32)
+            nc.scalar.activation(out=log_den[:], in_=cn_new[:, 1, :, :], func=ACT.Ln, scale=2.0, bias=two_eps[:, 0:1])
+            inv_den = stage.tile([P, BT, DH], F32)
+            nc.scalar.activation(out=inv_den[:], in_=log_den[:], func=ACT.Exp, scale=-1.0)
+            h_new = stage.tile([P, BT, DH], F32)
+            nc.vector.tensor_tensor(out=h_new[:], in0=oc_new[:], in1=inv_den[:], op=ALU.mult)
+
+            hcols = slice(head * DH, (head + 1) * DH)
+            nc.gpsimd.dma_start(out=batch_tiles(out_m)[:, :, hcols], in_=m_new[:])
+            nc.gpsimd.dma_start(out=batch_tiles(out_c)[:, :, hcols], in_=cn_new[:, 0, :, :])
+            nc.gpsimd.dma_start(out=batch_tiles(out_n)[:, :, hcols], in_=cn_new[:, 1, :, :])
+            nc.gpsimd.dma_start(out=batch_tiles(out_h)[:, :, hcols], in_=h_new[:])

@@ -24,6 +24,12 @@ KC = 4
 LN_EPS = 1e-5
 H_EPS = 1e-6
 GZ, GI, GF, GO = 0, 1, 2, 3
+WPH = 8
+N_WEIGHTS = WPH * NH
+RAW_BUFS = 6
+N_PAIRS = NT // 2
+CONV_LAG = 2
+PRO_STEPS = N_PAIRS + CONV_LAG
 
 FLOPS = 8 * 2 * B * D * DH
 
@@ -45,9 +51,9 @@ def tile_slstmblock_pa_kernel(
 
     with ExitStack() as stack:
         keep = stack.enter_context(tc.tile_pool(name="keep", bufs=1))
-        w_raw_pool = stack.enter_context(tc.tile_pool(name="w_raw", bufs=6))
+        w_raw_pool = stack.enter_context(tc.tile_pool(name="w_raw", bufs=RAW_BUFS))
         w_grp_pool = stack.enter_context(tc.tile_pool(name="w_grp", bufs=4))
-        w_mx_pool = stack.enter_context(tc.tile_pool(name="w_mx", bufs=2))
+        w_mx_pool = stack.enter_context(tc.tile_pool(name="w_mx", bufs=3))
 
         ident_f32 = keep.tile([P, P], F32)
         make_identity(nc, ident_f32[:])
@@ -69,42 +75,61 @@ def tile_slstmblock_pa_kernel(
         gate_bias = keep.tile([P, 4, NT], F32)
         half_o_bias = keep.tile([P, NT], F32)
 
-        def quantise_weight(w_head, pair_order, slot, on_vector):
-            raw = w_raw_pool.tile([P, PACK, DH], BF16)
-            if pair_order:
-                nc.sync.dma_start(
-                    out=raw[:].rearrange("q (u e) n -> q u (e n)", u=2),
-                    in_=w_head.rearrange("(u q e) n -> q u (e n)", u=2, e=2),
-                )
-            else:
-                nc.sync.dma_start(out=raw[:], in_=w_head.rearrange("(t p) n -> p t n", p=P))
-            grouped = w_grp_pool.tile([P, DH, PACK], BF16, align_bytes=64)
-            dst = grouped[:].rearrange("p (c i) t -> p c t i", i=4)
-            src = raw[:].rearrange("p t (c i) -> p c t i", i=4)
-            if on_vector:
-                nc.vector.tensor_copy(out=dst, in_=src)
-            else:
-                nc.scalar.copy(out=dst, in_=src)
-            codes = w_mx_pool.tile([P, DH], U32, tag="codes%d" % slot, align_bytes=64)
-            scales = w_mx_pool.tile([P, DH], U8, tag="scales%d" % slot, align_bytes=64)
-            nc.vector.quantize_mx(
-                out=codes[:].bitcast(FP8X4),
-                scales=scales[:],
-                in_=grouped[:].rearrange("p n t -> p (n t)"),
-            )
-            return codes, scales
-
         weight_list = []
         for gate in (GZ, GO, GI, GF):
             weight_list.append(("in", gate))
             weight_list.append(("rec", gate))
-        head_weights = [{} for head in range(NH)]
+        w_raw = {}
+        w_grouped = {}
+        w_mx = {}
 
-        def quantise_head_weight(head, slot):
-            kind, gate = weight_list[slot]
-            w = in_weights[gate] if kind == "in" else rec_weights[gate]
-            pair_order = not (kind == "in" and gate in (GI, GF))
-            head_weights[head][(kind, gate)] = quantise_weight(w[head], pair_order, slot, slot % 2 == 0)
+        def load_weight(w):
+            if w >= N_WEIGHTS:
+                return
+            kind, gate = weight_list[w % WPH]
+            w_head = (in_weights[gate] if kind == "in" else rec_weights[gate])[w // WPH]
+            raw = w_raw_pool.tile([P, PACK, DH], BF16)
+            if kind == "in" and gate in (GI, GF):
+                nc.sync.dma_start(out=raw[:], in_=w_head.rearrange("(t p) n -> p t n", p=P))
+            else:
+                nc.sync.dma_start(
+                    out=raw[:].rearrange("q (u e) n -> q u (e n)", u=2),
+                    in_=w_head.rearrange("(u q e) n -> q u (e n)", u=2, e=2),
+                )
+            w_raw[w] = raw
+
+        def regroup_weight(w):
+            if w >= N_WEIGHTS:
+                return
+            grouped = w_grp_pool.tile([P, DH, PACK], BF16, align_bytes=64)
+            dst = grouped[:].rearrange("p (c i) t -> p c t i", i=4)
+            src = w_raw[w][:].rearrange("p t (c i) -> p c t i", i=4)
+            if w % 2 == 0:
+                nc.vector.tensor_copy(out=dst, in_=src)
+            else:
+                nc.scalar.copy(out=dst, in_=src)
+            w_grouped[w] = grouped
+            load_weight(w + RAW_BUFS)
+
+        def quantise_weight(w):
+            if w < 0 or w >= N_WEIGHTS:
+                return
+            codes = w_mx_pool.tile([P, DH], U32, tag="codes%d" % (w % WPH), align_bytes=64)
+            scales = w_mx_pool.tile([P, DH], U8, tag="scales%d" % (w % WPH), align_bytes=64)
+            nc.vector.quantize_mx(
+                out=codes[:].bitcast(FP8X4),
+                scales=scales[:],
+                in_=w_grouped[w][:].rearrange("p n t -> p (n t)"),
+            )
+            w_mx[w] = (codes, scales)
+
+        def weights_first(step):
+            quantise_weight(2 * step - 1)
+            regroup_weight(2 * step)
+            regroup_weight(2 * step + 1)
+
+        def weights_second(step):
+            quantise_weight(2 * step)
 
         with tc.tile_pool(name="pro", bufs=1) as pro, tc.psum_pool(name="pro_psum", bufs=2) as pro_psum:
             x_sb = pro.tile([P, BT, D], BF16)
@@ -113,7 +138,11 @@ def tile_slstmblock_pa_kernel(
             for t in range(BT):
                 nc.sync.dma_start(out=x_sb[:, t, :], in_=x[t * P:(t + 1) * P, :])
             nc.sync.dma_start(out=h_sb[:], in_=batch_tiles(h_prev))
+            for w in range(RAW_BUFS):
+                load_weight(w)
             nc.sync.dma_start(out=m_sb[:], in_=batch_tiles(m_prev))
+            nc.sync.dma_start(out=cn_prev[:, 0, :, :], in_=batch_tiles(c_prev))
+            nc.sync.dma_start(out=cn_prev[:, 1, :, :], in_=batch_tiles(n_prev))
 
             bias_rows = pro.tile([P, P], BF16)
             ln_rows = pro.tile([P, P], BF16)
@@ -125,32 +154,6 @@ def tile_slstmblock_pa_kernel(
                     nc.gpsimd.dma_start(out=ln_rows[NT * v:NT * (v + 1), :], in_=vec.rearrange("(r c) -> r c", c=P))
                 nc.gpsimd.dma_start(out=taps_bf[:], in_=conv_w.partition_broadcast(P))
                 nc.gpsimd.dma_start(out=conv_bias_bf[:], in_=conv_b.partition_broadcast(P))
-                for v, vec in enumerate((wz_b, wi_b, wf_b, wo_b, rz_b, ri_b, rf_b, ro_b)):
-                    nc.gpsimd.dma_start(out=bias_rows[NT * v:NT * (v + 1), :], in_=vec.rearrange("(r c) -> r c", c=P))
-
-            taps = pro.tile([P, KC], F32)
-            nc.vector.tensor_copy(out=taps[:], in_=taps_bf[:])
-            conv_bias = pro.tile([P, 1], F32)
-            nc.vector.tensor_copy(out=conv_bias[:], in_=conv_bias_bf[:])
-
-            band = pro.tile([P, 2 * P], F32)
-            nc.vector.memset(band[:], 0.0)
-            for s in range(KC):
-                nc.vector.scalar_tensor_tensor(
-                    out=band[:, s:s + P], in0=ident_f32[:], scalar=taps[:, KC - 1 - s:KC - s],
-                    in1=band[:, s:s + P], op0=ALU.mult, op1=ALU.add,
-                )
-
-            vec_t = pro_psum.tile([P, 2, P], BF16, bufs=1)
-            nc.tensor.transpose(out=vec_t[:, 0, :], in_=bias_rows[:], identity=ident_bf[:])
-            nc.tensor.transpose(out=vec_t[:, 1, :], in_=ln_rows[:], identity=ident_bf[:])
-            vec_cols = pro.tile([P, 2, P], F32)
-            nc.vector.tensor_copy(out=vec_cols[:], in_=vec_t[:])
-            nc.vector.tensor_tensor(
-                out=gate_bias[:].rearrange("p g r -> p (g r)"),
-                in0=vec_cols[:, 0, 0:4 * NT], in1=vec_cols[:, 0, 4 * NT:8 * NT], op=ALU.add,
-            )
-            nc.vector.tensor_scalar_mul(out=half_o_bias[:], in0=gate_bias[:, GO, :], scalar1=0.5)
 
             stats = pro.tile([P, BT, NH, 6], F32)
             mean_var = pro.tile([P, BT, 2], F32)
@@ -163,18 +166,14 @@ def tile_slstmblock_pa_kernel(
                 nc.vector.bn_aggr(out=mean_var[:, t, :], in_=stats[:, t, :, :].rearrange("p c s -> p (c s)"))
                 nc.vector.tensor_scalar_add(out=var_eps[:, t:t + 1], in0=mean_var[:, t, 1:2], scalar1=LN_EPS)
                 nc.gpsimd.tensor_tensor(out=rstd[:, t:t + 1], in0=var_eps[:, t:t + 1], in1=minus_half[:], op=ALU.pow)
+            for t in range(BT):
                 nc.vector.scalar_tensor_tensor(
                     out=shift[:, t:t + 1], in0=mean_var[:, t, 0:1], scalar=-1.0, in1=rstd[:, t:t + 1],
                     op0=ALU.mult, op1=ALU.mult,
                 )
-            x_hat = pro.tile([P, BT, D], F32)
-            for head in range(NH):
-                for t in range(BT):
-                    cols = slice(head * DH, (head + 1) * DH)
-                    nc.scalar.activation(
-                        out=x_hat[:, t, cols], in_=x_sb[:, t, cols], func=ACT.Identity,
-                        scale=rstd[:, t:t + 1], bias=shift[:, t:t + 1],
-                    )
+            with nc.allow_non_contiguous_dma(reason="small vectors"):
+                for v, vec in enumerate((wz_b, wi_b, wf_b, wo_b, rz_b, ri_b, rf_b, ro_b)):
+                    nc.sync.dma_start(out=bias_rows[NT * v:NT * (v + 1), :], in_=vec.rearrange("(r c) -> r c", c=P))
 
             def transpose_pairs(src, name):
                 grouped = pro.tile([P, NH, B, PACK], BF16, name="grp_" + name, align_bytes=64)
@@ -192,6 +191,7 @@ def tile_slstmblock_pa_kernel(
                         out=grouped[:, head, :, :].bitcast(F32),
                         in_=words_t[:].rearrange("p u b -> p b u"),
                     )
+                for head in range(NH):
                     nc.vector.quantize_mx(
                         out=act_codes[name][:, head, :].bitcast(FP8X4),
                         scales=act_scales[name][:, head, :],
@@ -199,28 +199,66 @@ def tile_slstmblock_pa_kernel(
                     )
 
             transpose_pairs(x_sb, "x")
+            transpose_pairs(h_sb, "h")
 
+            taps = pro.tile([P, KC], F32)
+            nc.vector.tensor_copy(out=taps[:], in_=taps_bf[:])
+            conv_bias = pro.tile([P, 1], F32)
+            nc.vector.tensor_copy(out=conv_bias[:], in_=conv_bias_bf[:])
+            band = pro.tile([P, 2 * P], F32)
+            nc.vector.memset(band[:], 0.0)
+            for s in range(KC):
+                nc.vector.scalar_tensor_tensor(
+                    out=band[:, s:s + P], in0=ident_f32[:], scalar=taps[:, KC - 1 - s:KC - s],
+                    in1=band[:, s:s + P], op0=ALU.mult, op1=ALU.add,
+                )
+            ln_ps = pro_psum.tile([P, P], BF16, tag="vec_ps", bufs=1)
+            nc.tensor.transpose(out=ln_ps[:], in_=ln_rows[:], identity=ident_bf[:])
+            ln_cols = pro.tile([P, 2, NT], F32)
+            nc.vector.tensor_copy(out=ln_cols[:].rearrange("p v r -> p (v r)"), in_=ln_ps[:, 0:2 * NT])
+
+            x_hat = pro.tile([P, BT, D], F32)
             x_norm_t = pro.tile([P, NT, B], F32)
-            for pair in range(NT // 2):
-                x_hat_t = pro_psum.tile([P, 2, B], F32, tag="x_hat_t")
-                for i in range(2):
-                    r = 2 * pair + i
-                    for t in range(BT):
-                        nc.tensor.transpose(
-                            out=x_hat_t[:, i, t * P:(t + 1) * P], in_=x_hat[:, t, r * P:(r + 1) * P],
-                            identity=ident_f32[:],
-                        )
-                for i in range(2):
-                    r = 2 * pair + i
-                    nc.vector.tensor_scalar(
-                        out=x_norm_t[:, r, :], in0=x_hat_t[:, i, :],
-                        scalar1=vec_cols[:, 1, r:r + 1], scalar2=vec_cols[:, 1, NT + r:NT + r + 1],
-                        op0=ALU.mult, op1=ALU.add,
-                    )
-
             c_grouped = pro.tile([P, NH, B, PACK], BF16, align_bytes=64)
-            for head in range(NH):
-                for t in range(BT):
+
+            def quantise_x_conv(head):
+                nc.vector.quantize_mx(
+                    out=act_codes["c"][:, head, :].bitcast(FP8X4),
+                    scales=act_scales["c"][:, head, :],
+                    in_=c_grouped[:, head, :, :].rearrange("p b t -> p (b t)"),
+                )
+
+            for step in range(PRO_STEPS):
+                pair = step
+                bank = step - CONV_LAG
+                if pair < N_PAIRS:
+                    cols = slice(pair * 2 * P, (pair + 1) * 2 * P)
+                    for t in range(BT):
+                        nc.gpsimd.tensor_scalar(
+                            out=x_hat[:, t, cols], in0=x_sb[:, t, cols],
+                            scalar1=rstd[:, t:t + 1], scalar2=shift[:, t:t + 1], op0=ALU.mult, op1=ALU.add,
+                        )
+                weights_first(step)
+                if pair < N_PAIRS:
+                    x_hat_t = pro_psum.tile([P, 2, B], F32, tag="x_hat_t")
+                    for i in range(2):
+                        r = 2 * pair + i
+                        for t in range(BT):
+                            nc.tensor.transpose(
+                                out=x_hat_t[:, i, t * P:(t + 1) * P], in_=x_hat[:, t, r * P:(r + 1) * P],
+                                identity=ident_f32[:],
+                            )
+                    for i in range(2):
+                        r = 2 * pair + i
+                        nc.vector.tensor_scalar(
+                            out=x_norm_t[:, r, :], in0=x_hat_t[:, i, :],
+                            scalar1=ln_cols[:, 0, r:r + 1], scalar2=ln_cols[:, 1, r:r + 1],
+                            op0=ALU.mult, op1=ALU.add,
+                        )
+                if bank >= 1 and bank % BT == 0:
+                    quantise_x_conv(bank // BT - 1)
+                if bank >= 0:
+                    head, t = bank // BT, bank % BT
                     rows = slice(t * P, (t + 1) * P)
                     conv_t = pro_psum.tile([P, TPH, P], F32, tag="conv_t")
                     for j in range(TPH):
@@ -234,126 +272,184 @@ def tile_slstmblock_pa_kernel(
                                 out=conv_t[:, j, :], lhsT=band[:, P:2 * P], rhs=x_norm_t[:, r - 1, rows],
                                 start=False, stop=True,
                             )
+                weights_second(step)
+                if pair < N_PAIRS and pair % 2 == 1:
+                    m_head = pair // 2
+                    m_prev_ps = pro_psum.tile([P, TPH, B], BF16, bufs=1)
+                    for j in range(TPH):
+                        r = m_head * TPH + j
+                        for t in range(BT):
+                            nc.tensor.transpose(
+                                out=m_prev_ps[:, j, t * P:(t + 1) * P], in_=m_sb[:, t, r * P:(r + 1) * P],
+                                identity=ident_bf[:],
+                            )
+                    nc.scalar.copy(out=m_prev_t[:, m_head * TPH:(m_head + 1) * TPH, :], in_=m_prev_ps[:])
+                if bank >= 0:
                     nc.scalar.activation(
                         out=c_grouped[:, head, rows, :], in_=conv_t[:].rearrange("p j b -> p b j"),
                         func=ACT.Silu, bias=conv_bias[:, 0:1],
                     )
-                nc.vector.quantize_mx(
-                    out=act_codes["c"][:, head, :].bitcast(FP8X4),
-                    scales=act_scales["c"][:, head, :],
-                    in_=c_grouped[:, head, :, :].rearrange("p b t -> p (b t)"),
-                )
+            quantise_x_conv(NH - 1)
 
-            transpose_pairs(h_sb, "h")
-
-            for head in range(NH):
-                m_prev_ps = pro_psum.tile([P, TPH, B], BF16, bufs=1)
-                for j in range(TPH):
-                    r = head * TPH + j
-                    for t in range(BT):
-                        nc.tensor.transpose(
-                            out=m_prev_ps[:, j, t * P:(t + 1) * P], in_=m_sb[:, t, r * P:(r + 1) * P],
-                            identity=ident_bf[:],
-                        )
-                nc.scalar.copy(out=m_prev_t[:, head * TPH:(head + 1) * TPH, :], in_=m_prev_ps[:])
-
-        for slot in range(len(weight_list)):
-            quantise_head_weight(0, slot)
-        nc.sync.dma_start(out=cn_prev[:, 0, :, :], in_=batch_tiles(c_prev))
-        nc.sync.dma_start(out=cn_prev[:, 1, :, :], in_=batch_tiles(n_prev))
+            bias_ps = pro_psum.tile([P, P], BF16, tag="vec_ps", bufs=1)
+            nc.tensor.transpose(out=bias_ps[:], in_=bias_rows[:], identity=ident_bf[:])
+            bias_cols = pro.tile([P, P], F32)
+            nc.vector.tensor_copy(out=bias_cols[:], in_=bias_ps[:])
+            nc.vector.tensor_tensor(
+                out=gate_bias[:].rearrange("p g r -> p (g r)"),
+                in0=bias_cols[:, 0:4 * NT], in1=bias_cols[:, 4 * NT:8 * NT], op=ALU.add,
+            )
+            nc.vector.tensor_scalar_mul(out=half_o_bias[:], in0=gate_bias[:, GO, :], scalar1=0.5)
 
         work = stack.enter_context(tc.tile_pool(name="work", bufs=2))
         stage = stack.enter_context(tc.tile_pool(name="stage", bufs=2))
         gate_psum = stack.enter_context(tc.psum_pool(name="gate_psum", bufs=2))
         back_psum = stack.enter_context(tc.psum_pool(name="back_psum", bufs=1))
+        gates = {}
+        parts = {}
+        backs = {}
+        heads_out = {}
 
-        def gate_matmuls(out, head, gate, in_name, cols):
-            for kind, name, first in (("in", in_name, True), ("rec", "h", False)):
-                codes, scales = head_weights[head][(kind, gate)]
+        def gate_matmuls(out, r, gate, in_name):
+            head = r // TPH
+            cols = slice((r % TPH) * P, (r % TPH + 1) * P)
+            for kind, name in (("in", in_name), ("rec", "h")):
+                codes, scales = w_mx[head * WPH + weight_list.index((kind, gate))]
                 nc.tensor.matmul_mx(
                     out=out,
                     lhsT=codes[:, cols].bitcast(FP8X4), lhsT_scale=scales[:, cols],
                     rhs=act_codes[name][:, head, :].bitcast(FP8X4), rhs_scale=act_scales[name][:, head, :],
-                    start=first, stop=not first,
+                    start=(kind == "in"), stop=(kind == "rec"),
                 )
 
-        for head in range(NH):
-            cn_new = stage.tile([P, 2, BT, DH], F32)
-            oc_new = stage.tile([P, BT, DH], F32)
-            m_new = stage.tile([P, BT, DH], F32)
-            for j in range(TPH):
-                r = head * TPH + j
-                cols = slice(j * P, (j + 1) * P)
-                zo = gate_psum.tile([P, 2, B], F32)
-                gate_matmuls(zo[:, 0, :], head, GZ, "x", cols)
-                gate_matmuls(zo[:, 1, :], head, GO, "x", cols)
-                i_f = gate_psum.tile([P, 2, B], F32)
-                gate_matmuls(i_f[:, 0, :], head, GI, "c", cols)
-                gate_matmuls(i_f[:, 1, :], head, GF, "c", cols)
+        def matmuls(r):
+            zo = gate_psum.tile([P, 2, B], F32)
+            gate_matmuls(zo[:, 0, :], r, GZ, "x")
+            gate_matmuls(zo[:, 1, :], r, GO, "x")
+            i_f = gate_psum.tile([P, 2, B], F32)
+            gate_matmuls(i_f[:, 0, :], r, GI, "c")
+            gate_matmuls(i_f[:, 1, :], r, GF, "c")
+            gates[r] = (zo, i_f)
 
-                z = work.tile([P, B], F32)
-                nc.scalar.activation(out=z[:], in_=zo[:, 0, :], func=ACT.Tanh, bias=gate_bias[:, GZ, r:r + 1])
-                tanh_o = work.tile([P, B], F32)
-                nc.scalar.activation(
-                    out=tanh_o[:], in_=zo[:, 1, :], func=ACT.Tanh, bias=half_o_bias[:, r:r + 1], scale=0.5,
-                )
-                f_m = work.tile([P, B], F32)
-                nc.vector.scalar_tensor_tensor(
-                    out=f_m[:], in0=i_f[:, 1, :], scalar=gate_bias[:, GF, r:r + 1], in1=m_prev_t[:, r, :],
-                    op0=ALU.add, op1=ALU.add,
-                )
-                m_t = work.tile([P, B], F32)
-                nc.vector.scalar_tensor_tensor(
-                    out=m_t[:], in0=i_f[:, 0, :], scalar=gate_bias[:, GI, r:r + 1], in1=f_m[:],
-                    op0=ALU.add, op1=ALU.max,
-                )
-                below = work.tile([P, 2, B], F32)
-                nc.vector.scalar_tensor_tensor(
-                    out=below[:, 0, :], in0=i_f[:, 0, :], scalar=gate_bias[:, GI, r:r + 1], in1=m_t[:],
-                    op0=ALU.add, op1=ALU.subtract,
-                )
-                nc.vector.tensor_tensor(out=below[:, 1, :], in0=f_m[:], in1=m_t[:], op=ALU.subtract)
-                ig_fg = work.tile([P, 2, B], F32)
-                nc.scalar.activation(out=ig_fg[:], in_=below[:], func=ACT.Exp)
-                ig_z = work.tile([P, B], F32)
-                nc.vector.tensor_tensor(out=ig_z[:], in0=ig_fg[:, 0, :], in1=z[:], op=ALU.mult)
+        def stabilise(r):
+            i_f = gates[r][1]
+            f_m = work.tile([P, B], F32)
+            nc.vector.scalar_tensor_tensor(
+                out=f_m[:], in0=i_f[:, 1, :], scalar=gate_bias[:, GF, r:r + 1], in1=m_prev_t[:, r, :],
+                op0=ALU.add, op1=ALU.add,
+            )
+            m_t = work.tile([P, B], F32)
+            nc.vector.scalar_tensor_tensor(
+                out=m_t[:], in0=i_f[:, 0, :], scalar=gate_bias[:, GI, r:r + 1], in1=f_m[:],
+                op0=ALU.add, op1=ALU.max,
+            )
+            below = work.tile([P, 2, B], F32)
+            nc.vector.scalar_tensor_tensor(
+                out=below[:, 0, :], in0=i_f[:, 0, :], scalar=gate_bias[:, GI, r:r + 1], in1=m_t[:],
+                op0=ALU.add, op1=ALU.subtract,
+            )
+            nc.gpsimd.tensor_tensor(out=below[:, 1, :], in0=f_m[:], in1=m_t[:], op=ALU.subtract)
+            parts[r] = {"m_t": m_t, "below": below}
 
-                back_add = back_psum.tile([P, 2, BT, P], F32)
-                back_mul = back_psum.tile([P, 2, BT, P], F32)
-                back_m = back_psum.tile([P, BT, P], F32)
-                for t in range(BT):
-                    rows = slice(t * P, (t + 1) * P)
-                    nc.tensor.transpose(out=back_mul[:, 0, t, :], in_=ig_fg[:, 1, rows], identity=ident_f32[:])
-                    nc.tensor.transpose(out=back_add[:, 0, t, :], in_=ig_z[:, rows], identity=ident_f32[:])
-                    nc.tensor.transpose(out=back_add[:, 1, t, :], in_=ig_fg[:, 0, rows], identity=ident_f32[:])
-                    nc.tensor.transpose(out=back_mul[:, 1, t, :], in_=tanh_o[:, rows], identity=ident_f32[:])
-                    nc.tensor.transpose(out=back_m[:, t, :], in_=m_t[:, rows], identity=ident_f32[:])
+        def squash(r):
+            zo = gates[r][0]
+            z = work.tile([P, B], F32)
+            nc.scalar.activation(out=z[:], in_=zo[:, 0, :], func=ACT.Tanh, bias=gate_bias[:, GZ, r:r + 1])
+            tanh_o = work.tile([P, B], F32)
+            nc.scalar.activation(
+                out=tanh_o[:], in_=zo[:, 1, :], func=ACT.Tanh, bias=half_o_bias[:, r:r + 1], scale=0.5,
+            )
+            parts[r]["z"] = z
+            parts[r]["tanh_o"] = tanh_o
 
-                kept = work.tile([P, 2, BT, P], F32)
-                nc.vector.tensor_tensor(
-                    out=kept[:], in0=cn_prev[:, :, :, r * P:(r + 1) * P],
-                    in1=back_mul[:, 0:1, :, :].to_broadcast([P, 2, BT, P]), op=ALU.mult,
-                )
-                nc.vector.tensor_tensor(out=cn_new[:, :, :, cols], in0=kept[:], in1=back_add[:], op=ALU.add)
-                nc.vector.scalar_tensor_tensor(
-                    out=oc_new[:, :, cols], in0=back_mul[:, 1, :, :], scalar=1.0, in1=cn_new[:, 0, :, cols],
-                    op0=ALU.add, op1=ALU.mult,
-                )
-                nc.scalar.copy(out=m_new[:, :, cols], in_=back_m[:])
+        def exponentials(r):
+            ig_fg = work.tile([P, 2, B], F32)
+            nc.scalar.activation(out=ig_fg[:], in_=parts[r]["below"][:], func=ACT.Exp)
+            parts[r]["ig_fg"] = ig_fg
 
-                if head + 1 < NH:
-                    quantise_head_weight(head + 1, 2 * j)
-                    quantise_head_weight(head + 1, 2 * j + 1)
+        def input_term(r):
+            ig_z = work.tile([P, B], F32)
+            nc.gpsimd.tensor_tensor(out=ig_z[:], in0=parts[r]["ig_fg"][:, 0, :], in1=parts[r]["z"][:], op=ALU.mult)
+            parts[r]["ig_z"] = ig_z
 
+        def transpose_back(r):
+            back_add = back_psum.tile([P, 2, BT, P], F32)
+            back_mul = back_psum.tile([P, 2, BT, P], F32)
+            back_m = back_psum.tile([P, BT, P], F32)
+            part = parts[r]
+            for t in range(BT):
+                rows = slice(t * P, (t + 1) * P)
+                nc.tensor.transpose(out=back_mul[:, 0, t, :], in_=part["ig_fg"][:, 1, rows], identity=ident_f32[:])
+                nc.tensor.transpose(out=back_add[:, 0, t, :], in_=part["ig_z"][:, rows], identity=ident_f32[:])
+                nc.tensor.transpose(out=back_add[:, 1, t, :], in_=part["ig_fg"][:, 0, rows], identity=ident_f32[:])
+                nc.tensor.transpose(out=back_mul[:, 1, t, :], in_=part["tanh_o"][:, rows], identity=ident_f32[:])
+                nc.tensor.transpose(out=back_m[:, t, :], in_=part["m_t"][:, rows], identity=ident_f32[:])
+            backs[r] = (back_add, back_mul, back_m)
+
+        def update_state(r):
+            head = r // TPH
+            cols = slice((r % TPH) * P, (r % TPH + 1) * P)
+            if r % TPH == 0:
+                cn_new = stage.tile([P, 2, BT, DH], F32)
+                oc_new = stage.tile([P, BT, DH], F32)
+                m_new = stage.tile([P, BT, DH], F32)
+                heads_out[head] = {"cn": cn_new, "oc": oc_new, "m": m_new}
+            back_add, back_mul, back_m = backs[r]
+            outs = heads_out[head]
+            kept = work.tile([P, 2, BT, P], F32)
+            nc.vector.tensor_tensor(
+                out=kept[:], in0=cn_prev[:, :, :, r * P:(r + 1) * P],
+                in1=back_mul[:, 0:1, :, :].to_broadcast([P, 2, BT, P]), op=ALU.mult,
+            )
+            nc.vector.tensor_tensor(out=outs["cn"][:, :, :, cols], in0=kept[:], in1=back_add[:], op=ALU.add)
+            nc.vector.scalar_tensor_tensor(
+                out=outs["oc"][:, :, cols], in0=back_mul[:, 1, :, :], scalar=1.0, in1=outs["cn"][:, 0, :, cols],
+                op0=ALU.add, op1=ALU.mult,
+            )
+
+        def copy_m(r):
+            cols = slice((r % TPH) * P, (r % TPH + 1) * P)
+            nc.scalar.copy(out=heads_out[r // TPH]["m"][:, :, cols], in_=backs[r][2][:])
+
+        def reciprocal_of_n(head):
+            outs = heads_out[head]
             log_den = stage.tile([P, BT, DH], F32)
-            nc.scalar.activation(out=log_den[:], in_=cn_new[:, 1, :, :], func=ACT.Ln, scale=2.0, bias=two_eps[:, 0:1])
+            nc.scalar.activation(out=log_den[:], in_=outs["cn"][:, 1, :, :], func=ACT.Ln, scale=2.0, bias=two_eps[:, 0:1])
             inv_den = stage.tile([P, BT, DH], F32)
             nc.scalar.activation(out=inv_den[:], in_=log_den[:], func=ACT.Exp, scale=-1.0)
-            h_new = stage.tile([P, BT, DH], F32)
-            nc.vector.tensor_tensor(out=h_new[:], in0=oc_new[:], in1=inv_den[:], op=ALU.mult)
-
+            outs["inv_den"] = inv_den
             hcols = slice(head * DH, (head + 1) * DH)
-            nc.gpsimd.dma_start(out=batch_tiles(out_m)[:, :, hcols], in_=m_new[:])
-            nc.gpsimd.dma_start(out=batch_tiles(out_c)[:, :, hcols], in_=cn_new[:, 0, :, :])
-            nc.gpsimd.dma_start(out=batch_tiles(out_n)[:, :, hcols], in_=cn_new[:, 1, :, :])
-            nc.gpsimd.dma_start(out=batch_tiles(out_h)[:, :, hcols], in_=h_new[:])
+            nc.sync.dma_start(out=batch_tiles(out_m)[:, :, hcols], in_=outs["m"][:])
+            nc.sync.dma_start(out=batch_tiles(out_c)[:, :, hcols], in_=outs["cn"][:, 0, :, :])
+            nc.sync.dma_start(out=batch_tiles(out_n)[:, :, hcols], in_=outs["cn"][:, 1, :, :])
+
+        def finish_h(head):
+            outs = heads_out[head]
+            h_new = stage.tile([P, BT, DH], F32)
+            nc.vector.tensor_tensor(out=h_new[:], in0=outs["oc"][:], in1=outs["inv_den"][:], op=ALU.mult)
+            hcols = slice(head * DH, (head + 1) * DH)
+            nc.sync.dma_start(out=batch_tiles(out_h)[:, :, hcols], in_=h_new[:])
+
+        matmuls(0)
+        for r in range(NT + 2):
+            weights_first(PRO_STEPS + r)
+            if r + 1 < NT:
+                matmuls(r + 1)
+            if r < NT:
+                stabilise(r)
+            if 1 <= r <= NT:
+                update_state(r - 1)
+            if r < NT:
+                squash(r)
+            if 1 <= r <= NT:
+                copy_m(r - 1)
+            if r < NT:
+                exponentials(r)
+            weights_second(PRO_STEPS + r)
+            if r < NT:
+                input_term(r)
+                transpose_back(r)
+            if r > TPH and (r - 1) % TPH == 0:
+                finish_h((r - 1) // TPH - 1)
+            if r >= 1 and r % TPH == 0:
+                reciprocal_of_n(r // TPH - 1)

@@ -26,10 +26,12 @@ H_EPS = 1e-6
 GZ, GI, GF, GO = 0, 1, 2, 3
 WPH = 8
 N_WEIGHTS = WPH * NH
+RAW_FIRST = 6
 RAW_BUFS = 6
 N_PAIRS = NT // 2
-CONV_LAG = 2
-PRO_STEPS = N_PAIRS + CONV_LAG
+BANKS = NH * BT
+QUANT_LAG = 2
+BACK_LAG = 2
 
 FLOPS = 8 * 2 * B * D * DH
 
@@ -54,6 +56,9 @@ def tile_slstmblock_pa_kernel(
         w_raw_pool = stack.enter_context(tc.tile_pool(name="w_raw", bufs=RAW_BUFS))
         w_grp_pool = stack.enter_context(tc.tile_pool(name="w_grp", bufs=4))
         w_mx_pool = stack.enter_context(tc.tile_pool(name="w_mx", bufs=3))
+        psum = stack.enter_context(tc.psum_pool(name="psum", bufs=2))
+
+        stack.enter_context(tc.manual_schedule(engines={mybir.EngineType.Activation}))
 
         ident_f32 = keep.tile([P, P], F32)
         make_identity(nc, ident_f32[:])
@@ -63,6 +68,9 @@ def tile_slstmblock_pa_kernel(
         nc.vector.memset(minus_half[:], -0.5)
         two_eps = keep.tile([P, 1], F32)
         nc.vector.memset(two_eps[:], 2.0 * H_EPS)
+
+        table_warm = keep.tile([P, 1], F32)
+        nc.scalar.activation(out=table_warm[:], in_=two_eps[:], func=ACT.Silu)
 
         act_codes = {}
         act_scales = {}
@@ -83,12 +91,9 @@ def tile_slstmblock_pa_kernel(
         w_grouped = {}
         w_mx = {}
 
-        def load_weight(w):
-            if w >= N_WEIGHTS:
-                return
+        def load_weight(w, raw):
             kind, gate = weight_list[w % WPH]
             w_head = (in_weights[gate] if kind == "in" else rec_weights[gate])[w // WPH]
-            raw = w_raw_pool.tile([P, PACK, DH], BF16)
             if kind == "in" and gate in (GI, GF):
                 nc.sync.dma_start(out=raw[:], in_=w_head.rearrange("(t p) n -> p t n", p=P))
             else:
@@ -98,22 +103,27 @@ def tile_slstmblock_pa_kernel(
                 )
             w_raw[w] = raw
 
+        def load_ring(w):
+            if w < N_WEIGHTS:
+                raw = w_raw_pool.tile([P, PACK, DH], BF16)
+                load_weight(w, raw)
+
+        def on_vector(w):
+            return w % 2 == 0 and w % 16 != 14
+
         def regroup_weight(w):
-            if w >= N_WEIGHTS:
-                return
             grouped = w_grp_pool.tile([P, DH, PACK], BF16, align_bytes=64)
             dst = grouped[:].rearrange("p (c i) t -> p c t i", i=4)
             src = w_raw[w][:].rearrange("p t (c i) -> p c t i", i=4)
-            if w % 2 == 0:
+            if on_vector(w):
                 nc.vector.tensor_copy(out=dst, in_=src)
             else:
                 nc.scalar.copy(out=dst, in_=src)
             w_grouped[w] = grouped
-            load_weight(w + RAW_BUFS)
+            if w >= RAW_FIRST:
+                load_ring(w + RAW_BUFS)
 
         def quantise_weight(w):
-            if w < 0 or w >= N_WEIGHTS:
-                return
             codes = w_mx_pool.tile([P, DH], U32, tag="codes%d" % (w % WPH), align_bytes=64)
             scales = w_mx_pool.tile([P, DH], U8, tag="scales%d" % (w % WPH), align_bytes=64)
             nc.vector.quantize_mx(
@@ -123,26 +133,24 @@ def tile_slstmblock_pa_kernel(
             )
             w_mx[w] = (codes, scales)
 
-        def weights_first(step):
-            quantise_weight(2 * step - 1)
-            regroup_weight(2 * step)
-            regroup_weight(2 * step + 1)
+        taken = []
 
-        def weights_second(step):
-            quantise_weight(2 * step)
+        def take_weights(upto):
+            for w in range(len(taken), min(upto, N_WEIGHTS + QUANT_LAG)):
+                taken.append(w)
+                if w < N_WEIGHTS:
+                    regroup_weight(w)
+                if w >= QUANT_LAG:
+                    quantise_weight(w - QUANT_LAG)
 
-        with tc.tile_pool(name="pro", bufs=1) as pro, tc.psum_pool(name="pro_psum", bufs=2) as pro_psum:
+        with tc.tile_pool(name="pro", bufs=1) as pro:
             x_sb = pro.tile([P, BT, D], BF16)
             h_sb = pro.tile([P, BT, D], BF16)
             m_sb = pro.tile([P, BT, D], BF16)
-            for t in range(BT):
-                nc.sync.dma_start(out=x_sb[:, t, :], in_=x[t * P:(t + 1) * P, :])
-            nc.sync.dma_start(out=h_sb[:], in_=batch_tiles(h_prev))
-            for w in range(RAW_BUFS):
-                load_weight(w)
-            nc.sync.dma_start(out=m_sb[:], in_=batch_tiles(m_prev))
-            nc.sync.dma_start(out=cn_prev[:, 0, :, :], in_=batch_tiles(c_prev))
-            nc.sync.dma_start(out=cn_prev[:, 1, :, :], in_=batch_tiles(n_prev))
+
+            def load_first(w):
+                raw = pro.tile([P, PACK, DH], BF16, tag="raw_first", bufs=RAW_FIRST)
+                load_weight(w, raw)
 
             bias_rows = pro.tile([P, P], BF16)
             ln_rows = pro.tile([P, P], BF16)
@@ -151,55 +159,27 @@ def tile_slstmblock_pa_kernel(
             conv_bias_bf = pro.tile([P, 1], BF16)
             with nc.allow_non_contiguous_dma(reason="small vectors"):
                 for v, vec in enumerate((ln_g, ln_b)):
-                    nc.gpsimd.dma_start(out=ln_rows[NT * v:NT * (v + 1), :], in_=vec.rearrange("(r c) -> r c", c=P))
-                nc.gpsimd.dma_start(out=taps_bf[:], in_=conv_w.partition_broadcast(P))
-                nc.gpsimd.dma_start(out=conv_bias_bf[:], in_=conv_b.partition_broadcast(P))
+                    nc.sync.dma_start(out=ln_rows[NT * v:NT * (v + 1), :], in_=vec.rearrange("(r c) -> r c", c=P))
+                nc.sync.dma_start(out=taps_bf[:], in_=conv_w.partition_broadcast(P))
+                nc.sync.dma_start(out=conv_bias_bf[:], in_=conv_b.partition_broadcast(P))
 
-            stats = pro.tile([P, BT, NH, 6], F32)
-            mean_var = pro.tile([P, BT, 2], F32)
-            var_eps = pro.tile([P, BT], F32)
-            rstd = pro.tile([P, BT], F32)
-            shift = pro.tile([P, BT], F32)
+            for w in range(2):
+                load_first(w)
             for t in range(BT):
-                for head in range(NH):
-                    nc.vector.bn_stats(out=stats[:, t, head, :], in_=x_sb[:, t, head * DH:(head + 1) * DH])
-                nc.vector.bn_aggr(out=mean_var[:, t, :], in_=stats[:, t, :, :].rearrange("p c s -> p (c s)"))
-                nc.vector.tensor_scalar_add(out=var_eps[:, t:t + 1], in0=mean_var[:, t, 1:2], scalar1=LN_EPS)
-                nc.gpsimd.tensor_tensor(out=rstd[:, t:t + 1], in0=var_eps[:, t:t + 1], in1=minus_half[:], op=ALU.pow)
-            for t in range(BT):
-                nc.vector.scalar_tensor_tensor(
-                    out=shift[:, t:t + 1], in0=mean_var[:, t, 0:1], scalar=-1.0, in1=rstd[:, t:t + 1],
-                    op0=ALU.mult, op1=ALU.mult,
-                )
+                nc.sync.dma_start(out=x_sb[:, t, :], in_=x[t * P:(t + 1) * P, :])
+            for w in range(2, 4):
+                load_first(w)
+            nc.sync.dma_start(out=h_sb[:], in_=batch_tiles(h_prev))
+            for w in range(4, RAW_FIRST):
+                load_first(w)
+            nc.sync.dma_start(out=m_sb[:], in_=batch_tiles(m_prev))
+            for w in range(RAW_FIRST, RAW_FIRST + RAW_BUFS):
+                load_ring(w)
+            nc.sync.dma_start(out=cn_prev[:, 0, :, :], in_=batch_tiles(c_prev))
+            nc.sync.dma_start(out=cn_prev[:, 1, :, :], in_=batch_tiles(n_prev))
             with nc.allow_non_contiguous_dma(reason="small vectors"):
                 for v, vec in enumerate((wz_b, wi_b, wf_b, wo_b, rz_b, ri_b, rf_b, ro_b)):
                     nc.sync.dma_start(out=bias_rows[NT * v:NT * (v + 1), :], in_=vec.rearrange("(r c) -> r c", c=P))
-
-            def transpose_pairs(src, name):
-                grouped = pro.tile([P, NH, B, PACK], BF16, name="grp_" + name, align_bytes=64)
-                for head in range(NH):
-                    words_t = pro_psum.tile([P, 2, B], F32, tag="words_t")
-                    for u in range(2):
-                        for t in range(BT):
-                            first = head * (DH // 2) + u * P
-                            nc.tensor.transpose(
-                                out=words_t[:, u, t * P:(t + 1) * P],
-                                in_=src[:, t, :].bitcast(F32)[:, first:first + P],
-                                identity=ident_f32[:],
-                            )
-                    nc.scalar.copy(
-                        out=grouped[:, head, :, :].bitcast(F32),
-                        in_=words_t[:].rearrange("p u b -> p b u"),
-                    )
-                for head in range(NH):
-                    nc.vector.quantize_mx(
-                        out=act_codes[name][:, head, :].bitcast(FP8X4),
-                        scales=act_scales[name][:, head, :],
-                        in_=grouped[:, head, :, :].rearrange("p b t -> p (b t)"),
-                    )
-
-            transpose_pairs(x_sb, "x")
-            transpose_pairs(h_sb, "h")
 
             taps = pro.tile([P, KC], F32)
             nc.vector.tensor_copy(out=taps[:], in_=taps_bf[:])
@@ -212,99 +192,196 @@ def tile_slstmblock_pa_kernel(
                     out=band[:, s:s + P], in0=ident_f32[:], scalar=taps[:, KC - 1 - s:KC - s],
                     in1=band[:, s:s + P], op0=ALU.mult, op1=ALU.add,
                 )
-            ln_ps = pro_psum.tile([P, P], BF16, tag="vec_ps", bufs=1)
+            ln_ps = psum.tile([P, P], BF16, tag="m_zo")
             nc.tensor.transpose(out=ln_ps[:], in_=ln_rows[:], identity=ident_bf[:])
             ln_cols = pro.tile([P, 2, NT], F32)
             nc.vector.tensor_copy(out=ln_cols[:].rearrange("p v r -> p (v r)"), in_=ln_ps[:, 0:2 * NT])
 
-            x_hat = pro.tile([P, BT, D], F32)
-            x_norm_t = pro.tile([P, NT, B], F32)
-            c_grouped = pro.tile([P, NH, B, PACK], BF16, align_bytes=64)
+            stats = pro.tile([P, BT, NH, 6], F32)
+            mean_var = pro.tile([P, BT, 2], F32)
+            var_eps = pro.tile([P, BT], F32)
+            rstd = pro.tile([P, BT], F32)
+            shift = pro.tile([P, BT], F32)
+
+            def statistics():
+                for t in range(BT):
+                    for head in range(NH):
+                        nc.vector.bn_stats(out=stats[:, t, head, :], in_=x_sb[:, t, head * DH:(head + 1) * DH])
+                    nc.vector.bn_aggr(out=mean_var[:, t, :], in_=stats[:, t, :, :].rearrange("p c s -> p (c s)"))
+                    nc.vector.tensor_scalar_add(out=var_eps[:, t:t + 1], in0=mean_var[:, t, 1:2], scalar1=LN_EPS)
+                    nc.gpsimd.tensor_tensor(out=rstd[:, t:t + 1], in0=var_eps[:, t:t + 1], in1=minus_half[:], op=ALU.pow)
+
+            def finish_statistics():
+                for t in range(BT):
+                    nc.vector.scalar_tensor_tensor(
+                        out=shift[:, t:t + 1], in0=mean_var[:, t, 0:1], scalar=-1.0, in1=rstd[:, t:t + 1],
+                        op0=ALU.mult, op1=ALU.mult,
+                    )
+
+            x_norm_t = {}
+
+            x_hat = {}
+
+            def standardise(pair):
+                cols = slice(pair * 2 * P, (pair + 1) * 2 * P)
+                hat = pro.tile([P, BT, 2 * P], F32, bufs=4)
+                for t in range(BT):
+                    nc.gpsimd.tensor_scalar(
+                        out=hat[:, t, :], in0=x_sb[:, t, cols],
+                        scalar1=rstd[:, t:t + 1], scalar2=shift[:, t:t + 1], op0=ALU.mult, op1=ALU.add,
+                    )
+                x_hat[pair] = hat
+
+            x_hat_t = {}
+
+            def turn(pair):
+                hat_t = psum.tile([P, 2, B], F32, tag="norm_add")
+                for i in range(2):
+                    for t in range(BT):
+                        nc.tensor.transpose(
+                            out=hat_t[:, i, t * P:(t + 1) * P], in_=x_hat[pair][:, t, i * P:(i + 1) * P],
+                            identity=ident_f32[:],
+                        )
+                x_hat_t[pair] = hat_t
+
+            def gain_and_bias(pair):
+                x_norm = pro.tile([P, 2, B], F32, bufs=N_PAIRS)
+                for i in range(2):
+                    r = 2 * pair + i
+                    nc.vector.tensor_scalar(
+                        out=x_norm[:, i, :], in0=x_hat_t[pair][:, i, :],
+                        scalar1=ln_cols[:, 0, r:r + 1], scalar2=ln_cols[:, 1, r:r + 1],
+                        op0=ALU.mult, op1=ALU.add,
+                    )
+                x_norm_t[pair] = x_norm
+
+            c_grouped = {}
+            conv_out = {}
+
+            def convolve(bank):
+                head, t = bank // BT, bank % BT
+                if t == 0:
+                    grouped = pro.tile([P, B, PACK], BF16, align_bytes=64, bufs=2, name="c_grouped")
+                    c_grouped[head] = grouped
+                rows = slice(t * P, (t + 1) * P)
+                conv_t = psum.tile([P, TPH, P], F32, tag="conv_mul")
+                for j in range(TPH):
+                    r = head * TPH + j
+                    nc.tensor.matmul(
+                        out=conv_t[:, j, :], lhsT=band[:, 0:P], rhs=x_norm_t[r // 2][:, r % 2, rows],
+                        start=True, stop=(r == 0),
+                    )
+                    if r > 0:
+                        nc.tensor.matmul(
+                            out=conv_t[:, j, :], lhsT=band[:, P:2 * P],
+                            rhs=x_norm_t[(r - 1) // 2][:, (r - 1) % 2, rows],
+                            start=False, stop=True,
+                        )
+                conv_out[bank] = conv_t
+
+            def silu(bank):
+                head, t = bank // BT, bank % BT
+                nc.scalar.activation(
+                    out=c_grouped[head][:, t * P:(t + 1) * P, :], in_=conv_out[bank][:].rearrange("p j b -> p b j"),
+                    func=ACT.Silu, bias=conv_bias[:, 0:1],
+                )
 
             def quantise_x_conv(head):
                 nc.vector.quantize_mx(
                     out=act_codes["c"][:, head, :].bitcast(FP8X4),
                     scales=act_scales["c"][:, head, :],
-                    in_=c_grouped[:, head, :, :].rearrange("p b t -> p (b t)"),
+                    in_=c_grouped[head][:].rearrange("p b t -> p (b t)"),
                 )
 
-            for step in range(PRO_STEPS):
-                pair = step
-                bank = step - CONV_LAG
-                if pair < N_PAIRS:
-                    cols = slice(pair * 2 * P, (pair + 1) * 2 * P)
+            words = {}
+
+            def transpose_words(src, name, head):
+                grouped = pro.tile([P, B, PACK], BF16, align_bytes=64, bufs=6)
+                words_t = psum.tile([P, 2, B], F32, tag="words_if")
+                for u in range(2):
                     for t in range(BT):
-                        nc.gpsimd.tensor_scalar(
-                            out=x_hat[:, t, cols], in0=x_sb[:, t, cols],
-                            scalar1=rstd[:, t:t + 1], scalar2=shift[:, t:t + 1], op0=ALU.mult, op1=ALU.add,
+                        first = head * (DH // 2) + u * P
+                        nc.tensor.transpose(
+                            out=words_t[:, u, t * P:(t + 1) * P],
+                            in_=src[:, t, :].bitcast(F32)[:, first:first + P],
+                            identity=ident_f32[:],
                         )
-                weights_first(step)
-                if pair < N_PAIRS:
-                    x_hat_t = pro_psum.tile([P, 2, B], F32, tag="x_hat_t")
-                    for i in range(2):
-                        r = 2 * pair + i
-                        for t in range(BT):
-                            nc.tensor.transpose(
-                                out=x_hat_t[:, i, t * P:(t + 1) * P], in_=x_hat[:, t, r * P:(r + 1) * P],
-                                identity=ident_f32[:],
-                            )
-                    for i in range(2):
-                        r = 2 * pair + i
-                        nc.vector.tensor_scalar(
-                            out=x_norm_t[:, r, :], in0=x_hat_t[:, i, :],
-                            scalar1=ln_cols[:, 0, r:r + 1], scalar2=ln_cols[:, 1, r:r + 1],
-                            op0=ALU.mult, op1=ALU.add,
-                        )
-                if bank >= 1 and bank % BT == 0:
-                    quantise_x_conv(bank // BT - 1)
-                if bank >= 0:
-                    head, t = bank // BT, bank % BT
-                    rows = slice(t * P, (t + 1) * P)
-                    conv_t = pro_psum.tile([P, TPH, P], F32, tag="conv_t")
-                    for j in range(TPH):
-                        r = head * TPH + j
-                        nc.tensor.matmul(
-                            out=conv_t[:, j, :], lhsT=band[:, 0:P], rhs=x_norm_t[:, r, rows],
-                            start=True, stop=(r == 0),
-                        )
-                        if r > 0:
-                            nc.tensor.matmul(
-                                out=conv_t[:, j, :], lhsT=band[:, P:2 * P], rhs=x_norm_t[:, r - 1, rows],
-                                start=False, stop=True,
-                            )
-                weights_second(step)
-                if pair < N_PAIRS and pair % 2 == 1:
-                    m_head = pair // 2
-                    m_prev_ps = pro_psum.tile([P, TPH, B], BF16, bufs=1)
-                    for j in range(TPH):
-                        r = m_head * TPH + j
-                        for t in range(BT):
-                            nc.tensor.transpose(
-                                out=m_prev_ps[:, j, t * P:(t + 1) * P], in_=m_sb[:, t, r * P:(r + 1) * P],
-                                identity=ident_bf[:],
-                            )
-                    nc.scalar.copy(out=m_prev_t[:, m_head * TPH:(m_head + 1) * TPH, :], in_=m_prev_ps[:])
-                if bank >= 0:
-                    nc.scalar.activation(
-                        out=c_grouped[:, head, rows, :], in_=conv_t[:].rearrange("p j b -> p b j"),
-                        func=ACT.Silu, bias=conv_bias[:, 0:1],
-                    )
-            quantise_x_conv(NH - 1)
+                nc.scalar.copy(
+                    out=grouped[:].bitcast(F32),
+                    in_=words_t[:].rearrange("p u b -> p b u"),
+                )
+                words[name, head] = grouped
 
-            bias_ps = pro_psum.tile([P, P], BF16, tag="vec_ps", bufs=1)
-            nc.tensor.transpose(out=bias_ps[:], in_=bias_rows[:], identity=ident_bf[:])
-            bias_cols = pro.tile([P, P], F32)
-            nc.vector.tensor_copy(out=bias_cols[:], in_=bias_ps[:])
-            nc.vector.tensor_tensor(
-                out=gate_bias[:].rearrange("p g r -> p (g r)"),
-                in0=bias_cols[:, 0:4 * NT], in1=bias_cols[:, 4 * NT:8 * NT], op=ALU.add,
-            )
-            nc.vector.tensor_scalar_mul(out=half_o_bias[:], in0=gate_bias[:, GO, :], scalar1=0.5)
+            def quantise_words(name, head):
+                nc.vector.quantize_mx(
+                    out=act_codes[name][:, head, :].bitcast(FP8X4),
+                    scales=act_scales[name][:, head, :],
+                    in_=words[name, head][:].rearrange("p b t -> p (b t)"),
+                )
 
-        work = stack.enter_context(tc.tile_pool(name="work", bufs=2))
+            def transpose_m(head):
+                m_prev_ps = psum.tile([P, TPH, B], BF16, tag="m_zo")
+                for j in range(TPH):
+                    r = head * TPH + j
+                    for t in range(BT):
+                        nc.tensor.transpose(
+                            out=m_prev_ps[:, j, t * P:(t + 1) * P], in_=m_sb[:, t, r * P:(r + 1) * P],
+                            identity=ident_bf[:],
+                        )
+                nc.scalar.copy(out=m_prev_t[:, head * TPH:(head + 1) * TPH, :], in_=m_prev_ps[:])
+
+            def sum_biases():
+                bias_ps = psum.tile([P, P], BF16, tag="m_zo")
+                nc.tensor.transpose(out=bias_ps[:], in_=bias_rows[:], identity=ident_bf[:])
+                bias_cols = pro.tile([P, P], F32)
+                nc.vector.tensor_copy(out=bias_cols[:], in_=bias_ps[:])
+                nc.vector.tensor_tensor(
+                    out=gate_bias[:].rearrange("p g r -> p (g r)"),
+                    in0=bias_cols[:, 0:4 * NT], in1=bias_cols[:, 4 * NT:8 * NT], op=ALU.add,
+                )
+                nc.vector.tensor_scalar_mul(out=half_o_bias[:], in0=gate_bias[:, GO, :], scalar1=0.5)
+
+            take_weights(2)
+            statistics()
+            for head in range(NH):
+                transpose_words(x_sb, "x", head)
+            finish_statistics()
+            take_weights(3)
+            for pair in range(4):
+                standardise(pair)
+            for head in range(NH):
+                quantise_words("x", head)
+            turn(0)
+            take_weights(4)
+            turn(1)
+            gain_and_bias(0)
+            take_weights(6)
+            gain_and_bias(1)
+            turn(2)
+            for head in range(NH):
+                transpose_words(h_sb, "h", head)
+            gain_and_bias(2)
+            for bank in range(BANKS):
+                if bank + 4 < N_PAIRS:
+                    standardise(bank + 4)
+                if bank + 3 < N_PAIRS:
+                    turn(bank + 3)
+                convolve(bank)
+                take_weights(7 + bank + bank // 4)
+                if bank < NH:
+                    quantise_words("h", bank)
+                if bank % 2 == 0 and bank > 0:
+                    quantise_x_conv(bank // 2 - 1)
+                if bank + 3 < N_PAIRS:
+                    gain_and_bias(bank + 3)
+                silu(bank)
+                if 2 <= bank < 2 + NH:
+                    transpose_m(bank - 2)
+                if bank == BANKS - 2:
+                    sum_biases()
+
+        work = stack.enter_context(tc.tile_pool(name="work", bufs=3))
         stage = stack.enter_context(tc.tile_pool(name="stage", bufs=2))
-        gate_psum = stack.enter_context(tc.psum_pool(name="gate_psum", bufs=2))
-        back_psum = stack.enter_context(tc.psum_pool(name="back_psum", bufs=1))
         gates = {}
         parts = {}
         backs = {}
@@ -323,10 +400,10 @@ def tile_slstmblock_pa_kernel(
                 )
 
         def matmuls(r):
-            zo = gate_psum.tile([P, 2, B], F32)
+            zo = psum.tile([P, 2, B], F32, tag="m_zo")
             gate_matmuls(zo[:, 0, :], r, GZ, "x")
             gate_matmuls(zo[:, 1, :], r, GO, "x")
-            i_f = gate_psum.tile([P, 2, B], F32)
+            i_f = psum.tile([P, 2, B], F32, tag="words_if")
             gate_matmuls(i_f[:, 0, :], r, GI, "c")
             gate_matmuls(i_f[:, 1, :], r, GF, "c")
             gates[r] = (zo, i_f)
@@ -338,18 +415,14 @@ def tile_slstmblock_pa_kernel(
                 out=f_m[:], in0=i_f[:, 1, :], scalar=gate_bias[:, GF, r:r + 1], in1=m_prev_t[:, r, :],
                 op0=ALU.add, op1=ALU.add,
             )
-            m_t = work.tile([P, B], F32)
+            d = work.tile([P, B], F32)
             nc.vector.scalar_tensor_tensor(
-                out=m_t[:], in0=i_f[:, 0, :], scalar=gate_bias[:, GI, r:r + 1], in1=f_m[:],
-                op0=ALU.add, op1=ALU.max,
-            )
-            below = work.tile([P, 2, B], F32)
-            nc.vector.scalar_tensor_tensor(
-                out=below[:, 0, :], in0=i_f[:, 0, :], scalar=gate_bias[:, GI, r:r + 1], in1=m_t[:],
+                out=d[:], in0=i_f[:, 0, :], scalar=gate_bias[:, GI, r:r + 1], in1=f_m[:],
                 op0=ALU.add, op1=ALU.subtract,
             )
-            nc.gpsimd.tensor_tensor(out=below[:, 1, :], in0=f_m[:], in1=m_t[:], op=ALU.subtract)
-            parts[r] = {"m_t": m_t, "below": below}
+            drop = work.tile([P, B], F32)
+            nc.vector.tensor_scalar(out=drop[:], in0=d[:], scalar1=-1.0, scalar2=0.0, op0=ALU.mult, op1=ALU.max)
+            parts[r] = {"f_m": f_m, "d": d, "drop": drop}
 
         def squash(r):
             zo = gates[r][0]
@@ -363,43 +436,55 @@ def tile_slstmblock_pa_kernel(
             parts[r]["tanh_o"] = tanh_o
 
         def exponentials(r):
-            ig_fg = work.tile([P, 2, B], F32)
-            nc.scalar.activation(out=ig_fg[:], in_=parts[r]["below"][:], func=ACT.Exp)
-            parts[r]["ig_fg"] = ig_fg
-
-        def input_term(r):
+            part = parts[r]
+            fg = work.tile([P, B], F32)
+            nc.scalar.activation(out=fg[:], in_=part["d"][:], func=ACT.Exp, scale=-1.0)
+            ig = work.tile([P, B], F32)
+            nc.scalar.activation(out=ig[:], in_=part["drop"][:], func=ACT.Exp, scale=-1.0)
             ig_z = work.tile([P, B], F32)
-            nc.gpsimd.tensor_tensor(out=ig_z[:], in0=parts[r]["ig_fg"][:, 0, :], in1=parts[r]["z"][:], op=ALU.mult)
-            parts[r]["ig_z"] = ig_z
+            nc.gpsimd.tensor_tensor(out=ig_z[:], in0=ig[:], in1=part["z"][:], op=ALU.mult)
+            part["fg"], part["ig"], part["ig_z"] = fg, ig, ig_z
 
         def transpose_back(r):
-            back_add = back_psum.tile([P, 2, BT, P], F32)
-            back_mul = back_psum.tile([P, 2, BT, P], F32)
-            back_m = back_psum.tile([P, BT, P], F32)
+            back_mul = psum.tile([P, 2, BT, P], F32, tag="conv_mul")
+            back_add = psum.tile([P, 2, BT, P], F32, tag="norm_add")
+            if r % 2 == 0:
+                back_m = psum.tile([P, 2, BT, P], F32, tag="m_zo")
+            else:
+                back_m = backs[r - 1][2]
             part = parts[r]
+
+            def back(out, names, t):
+                for v, name in enumerate(names):
+                    nc.tensor.matmul(
+                        out=out, lhsT=part[name][:, t * P:(t + 1) * P], rhs=ident_f32[:], is_transpose=True,
+                        start=(v == 0), stop=(v == len(names) - 1),
+                    )
+
             for t in range(BT):
-                rows = slice(t * P, (t + 1) * P)
-                nc.tensor.transpose(out=back_mul[:, 0, t, :], in_=part["ig_fg"][:, 1, rows], identity=ident_f32[:])
-                nc.tensor.transpose(out=back_add[:, 0, t, :], in_=part["ig_z"][:, rows], identity=ident_f32[:])
-                nc.tensor.transpose(out=back_add[:, 1, t, :], in_=part["ig_fg"][:, 0, rows], identity=ident_f32[:])
-                nc.tensor.transpose(out=back_mul[:, 1, t, :], in_=part["tanh_o"][:, rows], identity=ident_f32[:])
-                nc.tensor.transpose(out=back_m[:, t, :], in_=part["m_t"][:, rows], identity=ident_f32[:])
+                back(back_m[:, r % 2, t, :], ("f_m", "d", "drop"), t)
+            for t in range(BT):
+                back(back_mul[:, 0, t, :], ("fg",), t)
+                back(back_mul[:, 1, t, :], ("tanh_o",), t)
+            for t in range(BT):
+                back(back_add[:, 1, t, :], ("ig",), t)
+                back(back_add[:, 0, t, :], ("ig_z",), t)
             backs[r] = (back_add, back_mul, back_m)
 
         def update_state(r):
             head = r // TPH
             cols = slice((r % TPH) * P, (r % TPH + 1) * P)
             if r % TPH == 0:
-                cn_new = stage.tile([P, 2, BT, DH], F32)
-                oc_new = stage.tile([P, BT, DH], F32)
+                cn_new = stage.tile([P, 2, BT, DH], F32, bufs=NH)
+                oc_new = stage.tile([P, BT, DH], F32, bufs=NH)
                 m_new = stage.tile([P, BT, DH], F32)
                 heads_out[head] = {"cn": cn_new, "oc": oc_new, "m": m_new}
             back_add, back_mul, back_m = backs[r]
             outs = heads_out[head]
-            kept = work.tile([P, 2, BT, P], F32)
-            nc.vector.tensor_tensor(
-                out=kept[:], in0=cn_prev[:, :, :, r * P:(r + 1) * P],
-                in1=back_mul[:, 0:1, :, :].to_broadcast([P, 2, BT, P]), op=ALU.mult,
+            kept = work.tile([P, 2, BT, P], F32, bufs=2)
+            nc.vector.scalar_tensor_tensor(
+                out=kept[:], in0=back_mul[:, 0:1, :, :].to_broadcast([P, 2, BT, P]), scalar=1.0,
+                in1=cn_prev[:, :, :, r * P:(r + 1) * P], op0=ALU.min, op1=ALU.mult,
             )
             nc.vector.tensor_tensor(out=outs["cn"][:, :, :, cols], in0=kept[:], in1=back_add[:], op=ALU.add)
             nc.vector.scalar_tensor_tensor(
@@ -408,48 +493,60 @@ def tile_slstmblock_pa_kernel(
             )
 
         def copy_m(r):
-            cols = slice((r % TPH) * P, (r % TPH + 1) * P)
-            nc.scalar.copy(out=heads_out[r // TPH]["m"][:, :, cols], in_=backs[r][2][:])
+            cols = slice((r % TPH - 1) * P, (r % TPH + 1) * P)
+            nc.scalar.copy(
+                out=heads_out[r // TPH]["m"][:, :, cols].rearrange("p t (q c) -> p t q c", q=2),
+                in_=backs[r][2][:].rearrange("p q t c -> p t q c"),
+            )
 
-        def reciprocal_of_n(head):
+        def store_states(head):
             outs = heads_out[head]
-            log_den = stage.tile([P, BT, DH], F32)
-            nc.scalar.activation(out=log_den[:], in_=outs["cn"][:, 1, :, :], func=ACT.Ln, scale=2.0, bias=two_eps[:, 0:1])
-            inv_den = stage.tile([P, BT, DH], F32)
-            nc.scalar.activation(out=inv_den[:], in_=log_den[:], func=ACT.Exp, scale=-1.0)
-            outs["inv_den"] = inv_den
             hcols = slice(head * DH, (head + 1) * DH)
             nc.sync.dma_start(out=batch_tiles(out_m)[:, :, hcols], in_=outs["m"][:])
             nc.sync.dma_start(out=batch_tiles(out_c)[:, :, hcols], in_=outs["cn"][:, 0, :, :])
             nc.sync.dma_start(out=batch_tiles(out_n)[:, :, hcols], in_=outs["cn"][:, 1, :, :])
 
+        def log_of_n(head):
+            outs = heads_out[head]
+            n_new = outs["cn"][:, 1, :, :]
+            if head == NH - 1:
+                last_log = stage.tile([P, BT, DH], F32, bufs=1)
+                outs["log"] = last_log[:]
+            else:
+                outs["log"] = n_new
+            nc.scalar.activation(out=outs["log"], in_=n_new, func=ACT.Ln, scale=2.0, bias=two_eps[:, 0:1])
+
         def finish_h(head):
             outs = heads_out[head]
-            h_new = stage.tile([P, BT, DH], F32)
-            nc.vector.tensor_tensor(out=h_new[:], in0=outs["oc"][:], in1=outs["inv_den"][:], op=ALU.mult)
+            nc.scalar.activation(out=outs["log"], in_=outs["log"], func=ACT.Exp, scale=-1.0)
+            nc.vector.tensor_tensor(out=outs["oc"][:], in0=outs["oc"][:], in1=outs["log"], op=ALU.mult)
             hcols = slice(head * DH, (head + 1) * DH)
-            nc.sync.dma_start(out=batch_tiles(out_h)[:, :, hcols], in_=h_new[:])
+            nc.sync.dma_start(out=batch_tiles(out_h)[:, :, hcols], in_=outs["oc"][:])
 
         matmuls(0)
-        for r in range(NT + 2):
-            weights_first(PRO_STEPS + r)
-            if r + 1 < NT:
-                matmuls(r + 1)
+        for r in range(NT + BACK_LAG):
+            back = r - BACK_LAG
+            if r == NT:
+                for head in range(NH - 1):
+                    log_of_n(head)
             if r < NT:
                 stabilise(r)
-            if 1 <= r <= NT:
-                update_state(r - 1)
-            if r < NT:
                 squash(r)
-            if 1 <= r <= NT:
-                copy_m(r - 1)
+            if r + 1 < NT:
+                matmuls(r + 1)
+            take_weights(16 + 2 * r)
+            if r == 0:
+                quantise_x_conv(NH - 1)
             if r < NT:
                 exponentials(r)
-            weights_second(PRO_STEPS + r)
-            if r < NT:
-                input_term(r)
-                transpose_back(r)
-            if r > TPH and (r - 1) % TPH == 0:
-                finish_h((r - 1) // TPH - 1)
-            if r >= 1 and r % TPH == 0:
-                reciprocal_of_n(r // TPH - 1)
+            if back >= 0:
+                update_state(back)
+                if back % 2 == 1:
+                    copy_m(back)
+            if 0 <= r - BACK_LAG + 1 < NT:
+                transpose_back(r - BACK_LAG + 1)
+            if back >= 0 and back % TPH == TPH - 1:
+                store_states(back // TPH)
+        log_of_n(NH - 1)
+        for head in range(NH):
+            finish_h(head)

@@ -109,7 +109,7 @@ def tile_slstmblock_pa_kernel(
                 load_weight(w, raw)
 
         def on_vector(w):
-            return w % 2 == 0 and w % 16 != 14
+            return w % 2 == 0
 
         def regroup_weight(w):
             grouped = w_grp_pool.tile([P, DH, PACK], BF16, align_bytes=64)

@@ -54,11 +54,11 @@ def tile_slstmblock_pa_kernel(
     with ExitStack() as stack:
         keep = stack.enter_context(tc.tile_pool(name="keep", bufs=1))
         w_raw_pool = stack.enter_context(tc.tile_pool(name="w_raw", bufs=RAW_BUFS))
-        w_grp_pool = stack.enter_context(tc.tile_pool(name="w_grp", bufs=4))
+        w_grp_pool = stack.enter_context(tc.tile_pool(name="w_grp", bufs=3))
         w_mx_pool = stack.enter_context(tc.tile_pool(name="w_mx", bufs=3))
         psum = stack.enter_context(tc.psum_pool(name="psum", bufs=2))
 
-        stack.enter_context(tc.manual_schedule(engines={mybir.EngineType.Activation}))
+        stack.enter_context(tc.manual_schedule(engines={mybir.EngineType.Activation, mybir.EngineType.DVE}))
 
         ident_f32 = keep.tile([P, P], F32)
         make_identity(nc, ident_f32[:])
@@ -109,10 +109,12 @@ def tile_slstmblock_pa_kernel(
                 load_weight(w, raw)
 
         def on_vector(w):
-            return w % 2 == 0
+            return w % 4 != 3 if w < 2 * WPH else w % WPH in (0, 2, 4)
 
         def regroup_weight(w):
-            grouped = w_grp_pool.tile([P, DH, PACK], BF16, align_bytes=64)
+            grouped = w_grp_pool.tile(
+                [P, DH, PACK], BF16, align_bytes=64, tag="vector" if on_vector(w) else "scalar",
+            )
             dst = grouped[:].rearrange("p (c i) t -> p c t i", i=4)
             src = w_raw[w][:].rearrange("p t (c i) -> p c t i", i=4)
             if on_vector(w):
@@ -158,16 +160,13 @@ def tile_slstmblock_pa_kernel(
             taps_bf = pro.tile([P, KC], BF16)
             conv_bias_bf = pro.tile([P, 1], BF16)
             with nc.allow_non_contiguous_dma(reason="small vectors"):
-                for v, vec in enumerate((ln_g, ln_b)):
-                    nc.sync.dma_start(out=ln_rows[NT * v:NT * (v + 1), :], in_=vec.rearrange("(r c) -> r c", c=P))
                 nc.sync.dma_start(out=taps_bf[:], in_=conv_w.partition_broadcast(P))
                 nc.sync.dma_start(out=conv_bias_bf[:], in_=conv_b.partition_broadcast(P))
-
-            for w in range(2):
-                load_first(w)
-            for t in range(BT):
-                nc.sync.dma_start(out=x_sb[:, t, :], in_=x[t * P:(t + 1) * P, :])
-            for w in range(2, 4):
+                for t in range(BT):
+                    nc.sync.dma_start(out=x_sb[:, t, :], in_=x[t * P:(t + 1) * P, :])
+                for v, vec in enumerate((ln_g, ln_b)):
+                    nc.sync.dma_start(out=ln_rows[NT * v:NT * (v + 1), :], in_=vec.rearrange("(r c) -> r c", c=P))
+            for w in range(4):
                 load_first(w)
             nc.sync.dma_start(out=h_sb[:], in_=batch_tiles(h_prev))
             for w in range(4, RAW_FIRST):
@@ -192,11 +191,6 @@ def tile_slstmblock_pa_kernel(
                     out=band[:, s:s + P], in0=ident_f32[:], scalar=taps[:, KC - 1 - s:KC - s],
                     in1=band[:, s:s + P], op0=ALU.mult, op1=ALU.add,
                 )
-            ln_ps = psum.tile([P, P], BF16, tag="m_zo")
-            nc.tensor.transpose(out=ln_ps[:], in_=ln_rows[:], identity=ident_bf[:])
-            ln_cols = pro.tile([P, 2, NT], F32)
-            nc.vector.tensor_copy(out=ln_cols[:].rearrange("p v r -> p (v r)"), in_=ln_ps[:, 0:2 * NT])
-
             stats = pro.tile([P, BT, NH, 6], F32)
             mean_var = pro.tile([P, BT, 2], F32)
             var_eps = pro.tile([P, BT], F32)
@@ -210,6 +204,13 @@ def tile_slstmblock_pa_kernel(
                     nc.vector.bn_aggr(out=mean_var[:, t, :], in_=stats[:, t, :, :].rearrange("p c s -> p (c s)"))
                     nc.vector.tensor_scalar_add(out=var_eps[:, t:t + 1], in0=mean_var[:, t, 1:2], scalar1=LN_EPS)
                     nc.gpsimd.tensor_tensor(out=rstd[:, t:t + 1], in0=var_eps[:, t:t + 1], in1=minus_half[:], op=ALU.pow)
+
+            ln_cols = pro.tile([P, 2, NT], F32)
+
+            def gain_and_bias_columns():
+                ln_ps = psum.tile([P, P], BF16, tag="m_zo", bufs=1)
+                nc.tensor.transpose(out=ln_ps[:], in_=ln_rows[:], identity=ident_bf[:])
+                nc.vector.tensor_copy(out=ln_cols[:].rearrange("p v r -> p (v r)"), in_=ln_ps[:, 0:2 * NT])
 
             def finish_statistics():
                 for t in range(BT):
@@ -248,10 +249,9 @@ def tile_slstmblock_pa_kernel(
                 x_norm = pro.tile([P, 2, B], F32, bufs=N_PAIRS)
                 for i in range(2):
                     r = 2 * pair + i
-                    nc.vector.tensor_scalar(
-                        out=x_norm[:, i, :], in0=x_hat_t[pair][:, i, :],
-                        scalar1=ln_cols[:, 0, r:r + 1], scalar2=ln_cols[:, 1, r:r + 1],
-                        op0=ALU.mult, op1=ALU.add,
+                    nc.scalar.activation(
+                        out=x_norm[:, i, :], in_=x_hat_t[pair][:, i, :], func=ACT.Identity,
+                        scale=ln_cols[:, 0, r:r + 1], bias=ln_cols[:, 1, r:r + 1],
                     )
                 x_norm_t[pair] = x_norm
 
@@ -296,7 +296,7 @@ def tile_slstmblock_pa_kernel(
             words = {}
 
             def transpose_words(src, name, head):
-                grouped = pro.tile([P, B, PACK], BF16, align_bytes=64, bufs=6)
+                grouped = pro.tile([P, B, PACK], BF16, align_bytes=64, bufs=4)
                 words_t = psum.tile([P, 2, B], F32, tag="words_if")
                 for u in range(2):
                     for t in range(BT):
@@ -320,7 +320,7 @@ def tile_slstmblock_pa_kernel(
                 )
 
             def transpose_m(head):
-                m_prev_ps = psum.tile([P, TPH, B], BF16, tag="m_zo")
+                m_prev_ps = psum.tile([P, TPH, B], BF16, tag=("m_zo", "m_m")[head % 2], bufs=1)
                 for j in range(TPH):
                     r = head * TPH + j
                     for t in range(BT):
@@ -331,7 +331,7 @@ def tile_slstmblock_pa_kernel(
                 nc.scalar.copy(out=m_prev_t[:, head * TPH:(head + 1) * TPH, :], in_=m_prev_ps[:])
 
             def sum_biases():
-                bias_ps = psum.tile([P, P], BF16, tag="m_zo")
+                bias_ps = psum.tile([P, P], BF16, tag="norm_add")
                 nc.tensor.transpose(out=bias_ps[:], in_=bias_rows[:], identity=ident_bf[:])
                 bias_cols = pro.tile([P, P], F32)
                 nc.vector.tensor_copy(out=bias_cols[:], in_=bias_ps[:])
@@ -341,25 +341,25 @@ def tile_slstmblock_pa_kernel(
                 )
                 nc.vector.tensor_scalar_mul(out=half_o_bias[:], in0=gate_bias[:, GO, :], scalar1=0.5)
 
-            take_weights(2)
             statistics()
             for head in range(NH):
                 transpose_words(x_sb, "x", head)
+            take_weights(1)
+            gain_and_bias_columns()
             finish_statistics()
-            take_weights(3)
             for pair in range(4):
                 standardise(pair)
             for head in range(NH):
                 quantise_words("x", head)
-            turn(0)
             take_weights(4)
+            turn(0)
             turn(1)
             gain_and_bias(0)
-            take_weights(6)
             gain_and_bias(1)
-            turn(2)
             for head in range(NH):
                 transpose_words(h_sb, "h", head)
+            take_weights(6)
+            turn(2)
             gain_and_bias(2)
             for bank in range(BANKS):
                 if bank + 4 < N_PAIRS:
@@ -379,6 +379,7 @@ def tile_slstmblock_pa_kernel(
                     transpose_m(bank - 2)
                 if bank == BANKS - 2:
                     sum_biases()
+            quantise_x_conv(NH - 1)
 
         work = stack.enter_context(tc.tile_pool(name="work", bufs=3))
         stage = stack.enter_context(tc.tile_pool(name="stage", bufs=2))
@@ -400,7 +401,7 @@ def tile_slstmblock_pa_kernel(
                 )
 
         def matmuls(r):
-            zo = psum.tile([P, 2, B], F32, tag="m_zo")
+            zo = psum.tile([P, 2, B], F32, tag="m_zo", bufs=1)
             gate_matmuls(zo[:, 0, :], r, GZ, "x")
             gate_matmuls(zo[:, 1, :], r, GO, "x")
             i_f = psum.tile([P, 2, B], F32, tag="words_if")
@@ -408,21 +409,28 @@ def tile_slstmblock_pa_kernel(
             gate_matmuls(i_f[:, 1, :], r, GF, "c")
             gates[r] = (zo, i_f)
 
-        def stabilise(r):
-            i_f = gates[r][1]
+        def add_m_prev(r):
             f_m = work.tile([P, B], F32)
             nc.vector.scalar_tensor_tensor(
-                out=f_m[:], in0=i_f[:, 1, :], scalar=gate_bias[:, GF, r:r + 1], in1=m_prev_t[:, r, :],
+                out=f_m[:], in0=gates[r][1][:, 1, :], scalar=gate_bias[:, GF, r:r + 1], in1=m_prev_t[:, r, :],
                 op0=ALU.add, op1=ALU.add,
             )
+            parts[r] = {"f_m": f_m}
+
+        def difference(r):
             d = work.tile([P, B], F32)
             nc.vector.scalar_tensor_tensor(
-                out=d[:], in0=i_f[:, 0, :], scalar=gate_bias[:, GI, r:r + 1], in1=f_m[:],
+                out=d[:], in0=gates[r][1][:, 0, :], scalar=gate_bias[:, GI, r:r + 1], in1=parts[r]["f_m"][:],
                 op0=ALU.add, op1=ALU.subtract,
             )
+            parts[r]["d"] = d
+
+        def drop_of(r):
             drop = work.tile([P, B], F32)
-            nc.vector.tensor_scalar(out=drop[:], in0=d[:], scalar1=-1.0, scalar2=0.0, op0=ALU.mult, op1=ALU.max)
-            parts[r] = {"f_m": f_m, "d": d, "drop": drop}
+            nc.vector.tensor_scalar(
+                out=drop[:], in0=parts[r]["d"][:], scalar1=-1.0, scalar2=0.0, op0=ALU.mult, op1=ALU.max,
+            )
+            parts[r]["drop"] = drop
 
         def squash(r):
             zo = gates[r][0]
@@ -449,7 +457,7 @@ def tile_slstmblock_pa_kernel(
             back_mul = psum.tile([P, 2, BT, P], F32, tag="conv_mul")
             back_add = psum.tile([P, 2, BT, P], F32, tag="norm_add")
             if r % 2 == 0:
-                back_m = psum.tile([P, 2, BT, P], F32, tag="m_zo")
+                back_m = psum.tile([P, 2, BT, P], F32, tag="m_m", bufs=1)
             else:
                 back_m = backs[r - 1][2]
             part = parts[r]
@@ -471,30 +479,36 @@ def tile_slstmblock_pa_kernel(
                 back(back_add[:, 0, t, :], ("ig_z",), t)
             backs[r] = (back_add, back_mul, back_m)
 
-        def update_state(r):
-            head = r // TPH
-            cols = slice((r % TPH) * P, (r % TPH + 1) * P)
+        def keep_states(r):
             if r % TPH == 0:
                 cn_new = stage.tile([P, 2, BT, DH], F32, bufs=NH)
                 oc_new = stage.tile([P, BT, DH], F32, bufs=NH)
                 m_new = stage.tile([P, BT, DH], F32)
-                heads_out[head] = {"cn": cn_new, "oc": oc_new, "m": m_new}
-            back_add, back_mul, back_m = backs[r]
-            outs = heads_out[head]
+                heads_out[r // TPH] = {"cn": cn_new, "oc": oc_new, "m": m_new}
             kept = work.tile([P, 2, BT, P], F32, bufs=2)
             nc.vector.scalar_tensor_tensor(
-                out=kept[:], in0=back_mul[:, 0:1, :, :].to_broadcast([P, 2, BT, P]), scalar=1.0,
+                out=kept[:], in0=backs[r][1][:, 0:1, :, :].to_broadcast([P, 2, BT, P]), scalar=1.0,
                 in1=cn_prev[:, :, :, r * P:(r + 1) * P], op0=ALU.min, op1=ALU.mult,
             )
-            nc.vector.tensor_tensor(out=outs["cn"][:, :, :, cols], in0=kept[:], in1=back_add[:], op=ALU.add)
+            parts[r]["kept"] = kept
+
+        def add_inputs(r):
+            cols = slice((r % TPH) * P, (r % TPH + 1) * P)
+            nc.vector.tensor_tensor(
+                out=heads_out[r // TPH]["cn"][:, :, :, cols], in0=parts[r]["kept"][:], in1=backs[r][0][:], op=ALU.add,
+            )
+
+        def open_output(r):
+            outs = heads_out[r // TPH]
+            cols = slice((r % TPH) * P, (r % TPH + 1) * P)
             nc.vector.scalar_tensor_tensor(
-                out=outs["oc"][:, :, cols], in0=back_mul[:, 1, :, :], scalar=1.0, in1=outs["cn"][:, 0, :, cols],
+                out=outs["oc"][:, :, cols], in0=backs[r][1][:, 1, :, :], scalar=1.0, in1=outs["cn"][:, 0, :, cols],
                 op0=ALU.add, op1=ALU.mult,
             )
 
         def copy_m(r):
             cols = slice((r % TPH - 1) * P, (r % TPH + 1) * P)
-            nc.scalar.copy(
+            (nc.vector.tensor_copy if r == NT - 1 else nc.scalar.copy)(
                 out=heads_out[r // TPH]["m"][:, :, cols].rearrange("p t (q c) -> p t q c", q=2),
                 in_=backs[r][2][:].rearrange("p q t c -> p t q c"),
             )
@@ -530,19 +544,25 @@ def tile_slstmblock_pa_kernel(
                 for head in range(NH - 1):
                     log_of_n(head)
             if r < NT:
-                stabilise(r)
+                add_m_prev(r)
+            if back >= 0:
+                keep_states(back)
+            if r < NT:
+                difference(r)
                 squash(r)
+            if back >= 0:
+                add_inputs(back)
+            if r < NT:
+                drop_of(r)
+            if back >= 0:
+                open_output(back)
             if r + 1 < NT:
                 matmuls(r + 1)
             take_weights(16 + 2 * r)
-            if r == 0:
-                quantise_x_conv(NH - 1)
             if r < NT:
                 exponentials(r)
-            if back >= 0:
-                update_state(back)
-                if back % 2 == 1:
-                    copy_m(back)
+            if back >= 0 and back % 2 == 1:
+                copy_m(back)
             if 0 <= r - BACK_LAG + 1 < NT:
                 transpose_back(r - BACK_LAG + 1)
             if back >= 0 and back % TPH == TPH - 1:

@@ -31,7 +31,7 @@ RAW_BUFS = 6
 N_PAIRS = NT // 2
 BANKS = NH * BT
 QUANT_LAG = 2
-BACK_LAG = 2
+STEPS = NH * BT
 
 FLOPS = 8 * 2 * B * D * DH
 
@@ -55,10 +55,10 @@ def tile_slstmblock_pa_kernel(
         keep = stack.enter_context(tc.tile_pool(name="keep", bufs=1))
         w_raw_pool = stack.enter_context(tc.tile_pool(name="w_raw", bufs=RAW_BUFS))
         w_grp_pool = stack.enter_context(tc.tile_pool(name="w_grp", bufs=3))
-        w_mx_pool = stack.enter_context(tc.tile_pool(name="w_mx", bufs=3))
+        w_mx_pool = stack.enter_context(tc.tile_pool(name="w_mx", bufs=2))
         psum = stack.enter_context(tc.psum_pool(name="psum", bufs=2))
 
-        stack.enter_context(tc.manual_schedule(engines={mybir.EngineType.Activation, mybir.EngineType.DVE}))
+        stack.enter_context(tc.manual_schedule(engines={mybir.EngineType.Activation}))
 
         ident_f32 = keep.tile([P, P], F32)
         make_identity(nc, ident_f32[:])
@@ -78,10 +78,10 @@ def tile_slstmblock_pa_kernel(
             act_codes[name] = keep.tile([P, NH, B], U32, name="codes_" + name, align_bytes=64)
             act_scales[name] = keep.tile([P, NH, B], U8, name="scales_" + name, align_bytes=64)
 
-        m_prev_t = keep.tile([P, NT, B], BF16)
+        m_shift = keep.tile([P, BT, D], F32)
+        i_bias = keep.tile([P, D], F32)
         cn_prev = keep.tile([P, 2, BT, D], BF16)
-        gate_bias = keep.tile([P, 4, NT], F32)
-        half_o_bias = keep.tile([P, NT], F32)
+        zo_bias = keep.tile([P, 2, NT], F32)
 
         weight_list = []
         for gate in (GZ, GO, GI, GF):
@@ -109,7 +109,7 @@ def tile_slstmblock_pa_kernel(
                 load_weight(w, raw)
 
         def on_vector(w):
-            return w % 4 != 3 if w < 2 * WPH else w % WPH in (0, 2, 4)
+            return w not in (1, 3, 5, 7, 9) if w < 2 * WPH else w % WPH in (0, 2, 4)
 
         def regroup_weight(w):
             grouped = w_grp_pool.tile(
@@ -168,6 +168,9 @@ def tile_slstmblock_pa_kernel(
                     nc.sync.dma_start(out=ln_rows[NT * v:NT * (v + 1), :], in_=vec.rearrange("(r c) -> r c", c=P))
             for w in range(4):
                 load_first(w)
+            with nc.allow_non_contiguous_dma(reason="small vectors"):
+                for v, vec in enumerate((wz_b, wi_b, wf_b, wo_b, rz_b, ri_b, rf_b, ro_b)):
+                    nc.sync.dma_start(out=bias_rows[NT * v:NT * (v + 1), :], in_=vec.rearrange("(r c) -> r c", c=P))
             nc.sync.dma_start(out=h_sb[:], in_=batch_tiles(h_prev))
             for w in range(4, RAW_FIRST):
                 load_first(w)
@@ -176,9 +179,6 @@ def tile_slstmblock_pa_kernel(
                 load_ring(w)
             nc.sync.dma_start(out=cn_prev[:, 0, :, :], in_=batch_tiles(c_prev))
             nc.sync.dma_start(out=cn_prev[:, 1, :, :], in_=batch_tiles(n_prev))
-            with nc.allow_non_contiguous_dma(reason="small vectors"):
-                for v, vec in enumerate((wz_b, wi_b, wf_b, wo_b, rz_b, ri_b, rf_b, ro_b)):
-                    nc.sync.dma_start(out=bias_rows[NT * v:NT * (v + 1), :], in_=vec.rearrange("(r c) -> r c", c=P))
 
             taps = pro.tile([P, KC], F32)
             nc.vector.tensor_copy(out=taps[:], in_=taps_bf[:])
@@ -208,7 +208,7 @@ def tile_slstmblock_pa_kernel(
             ln_cols = pro.tile([P, 2, NT], F32)
 
             def gain_and_bias_columns():
-                ln_ps = psum.tile([P, P], BF16, tag="m_zo", bufs=1)
+                ln_ps = psum.tile([P, P], BF16, tag="vec_i", bufs=1)
                 nc.tensor.transpose(out=ln_ps[:], in_=ln_rows[:], identity=ident_bf[:])
                 nc.vector.tensor_copy(out=ln_cols[:].rearrange("p v r -> p (v r)"), in_=ln_ps[:, 0:2 * NT])
 
@@ -223,20 +223,20 @@ def tile_slstmblock_pa_kernel(
 
             x_hat = {}
 
-            def standardise(pair):
-                cols = slice(pair * 2 * P, (pair + 1) * 2 * P)
-                hat = pro.tile([P, BT, 2 * P], F32, bufs=4)
+            def standardise(head):
+                hat = pro.tile([P, BT, DH], F32, bufs=3)
                 for t in range(BT):
-                    nc.gpsimd.tensor_scalar(
-                        out=hat[:, t, :], in0=x_sb[:, t, cols],
+                    nc.vector.tensor_scalar(
+                        out=hat[:, t, :], in0=x_sb[:, t, head * DH:(head + 1) * DH],
                         scalar1=rstd[:, t:t + 1], scalar2=shift[:, t:t + 1], op0=ALU.mult, op1=ALU.add,
                     )
-                x_hat[pair] = hat
+                for half in range(2):
+                    x_hat[2 * head + half] = hat[:, :, half * 2 * P:(half + 1) * 2 * P]
 
             x_hat_t = {}
 
             def turn(pair):
-                hat_t = psum.tile([P, 2, B], F32, tag="norm_add")
+                hat_t = psum.tile([P, 2, B], F32, tag="norm_o")
                 for i in range(2):
                     for t in range(BT):
                         nc.tensor.transpose(
@@ -264,7 +264,7 @@ def tile_slstmblock_pa_kernel(
                     grouped = pro.tile([P, B, PACK], BF16, align_bytes=64, bufs=2, name="c_grouped")
                     c_grouped[head] = grouped
                 rows = slice(t * P, (t + 1) * P)
-                conv_t = psum.tile([P, TPH, P], F32, tag="conv_mul")
+                conv_t = psum.tile([P, TPH, P], F32, tag="conv_z")
                 for j in range(TPH):
                     r = head * TPH + j
                     nc.tensor.matmul(
@@ -297,7 +297,7 @@ def tile_slstmblock_pa_kernel(
 
             def transpose_words(src, name, head):
                 grouped = pro.tile([P, B, PACK], BF16, align_bytes=64, bufs=4)
-                words_t = psum.tile([P, 2, B], F32, tag="words_if")
+                words_t = psum.tile([P, 2, B], F32, tag="words_zo")
                 for u in range(2):
                     for t in range(BT):
                         first = head * (DH // 2) + u * P
@@ -319,36 +319,60 @@ def tile_slstmblock_pa_kernel(
                     in_=words[name, head][:].rearrange("p b t -> p (b t)"),
                 )
 
-            def transpose_m(head):
-                m_prev_ps = psum.tile([P, TPH, B], BF16, tag=("m_zo", "m_m")[head % 2], bufs=1)
-                for j in range(TPH):
-                    r = head * TPH + j
-                    for t in range(BT):
-                        nc.tensor.transpose(
-                            out=m_prev_ps[:, j, t * P:(t + 1) * P], in_=m_sb[:, t, r * P:(r + 1) * P],
-                            identity=ident_bf[:],
+            selector = pro.tile([P, 2, NT], BF16)
+
+            def make_selector():
+                f_rows = pro.tile([P, NT], BF16)
+                nc.vector.tensor_tensor(
+                    out=selector[:, 1, :], in0=ident_bf[:, GI * NT:(GI + 1) * NT],
+                    in1=ident_bf[:, (4 + GI) * NT:(5 + GI) * NT], op=ALU.add,
+                )
+                nc.vector.tensor_tensor(
+                    out=f_rows[:], in0=ident_bf[:, GF * NT:(GF + 1) * NT],
+                    in1=ident_bf[:, (4 + GF) * NT:(5 + GF) * NT], op=ALU.add,
+                )
+                nc.vector.tensor_tensor(out=selector[:, 0, :], in0=f_rows[:], in1=selector[:, 1, :], op=ALU.subtract)
+
+            def spread_biases(head):
+                hcols = slice(head * DH, (head + 1) * DH)
+                spread = []
+                for v, tag in enumerate(("vec_i", "vec_f")):
+                    rows = psum.tile([P, DH], F32, tag=tag, bufs=1, name="spread")
+                    for j in range(TPH):
+                        r = head * TPH + j
+                        nc.tensor.matmul(
+                            out=rows[:, j * P:(j + 1) * P], lhsT=selector[:, v, r:r + 1].to_broadcast([P, P]),
+                            rhs=bias_rows[:], start=True, stop=True,
                         )
-                nc.scalar.copy(out=m_prev_t[:, head * TPH:(head + 1) * TPH, :], in_=m_prev_ps[:])
+                    spread.append(rows)
+                nc.vector.tensor_tensor(
+                    out=m_shift[:, :, hcols], in0=m_sb[:, :, hcols],
+                    in1=spread[0][:].unsqueeze(1).to_broadcast([P, BT, DH]), op=ALU.add,
+                )
+                nc.scalar.copy(out=i_bias[:, hcols], in_=spread[1][:])
 
             def sum_biases():
-                bias_ps = psum.tile([P, P], BF16, tag="norm_add")
+                bias_ps = psum.tile([P, P], BF16, tag="norm_o")
                 nc.tensor.transpose(out=bias_ps[:], in_=bias_rows[:], identity=ident_bf[:])
                 bias_cols = pro.tile([P, P], F32)
                 nc.vector.tensor_copy(out=bias_cols[:], in_=bias_ps[:])
-                nc.vector.tensor_tensor(
-                    out=gate_bias[:].rearrange("p g r -> p (g r)"),
-                    in0=bias_cols[:, 0:4 * NT], in1=bias_cols[:, 4 * NT:8 * NT], op=ALU.add,
-                )
-                nc.vector.tensor_scalar_mul(out=half_o_bias[:], in0=gate_bias[:, GO, :], scalar1=0.5)
+                o_sum = pro.tile([P, NT], F32)
+                for out, gate in ((zo_bias[:, 0, :], GZ), (o_sum[:], GO)):
+                    nc.vector.tensor_tensor(
+                        out=out, in0=bias_cols[:, gate * NT:(gate + 1) * NT],
+                        in1=bias_cols[:, (4 + gate) * NT:(5 + gate) * NT], op=ALU.add,
+                    )
+                nc.vector.tensor_scalar_mul(out=zo_bias[:, 1, :], in0=o_sum[:], scalar1=0.5)
 
+            make_selector()
             statistics()
             for head in range(NH):
                 transpose_words(x_sb, "x", head)
             take_weights(1)
             gain_and_bias_columns()
             finish_statistics()
-            for pair in range(4):
-                standardise(pair)
+            for head in range(2):
+                standardise(head)
             for head in range(NH):
                 quantise_words("x", head)
             take_weights(4)
@@ -362,8 +386,8 @@ def tile_slstmblock_pa_kernel(
             turn(2)
             gain_and_bias(2)
             for bank in range(BANKS):
-                if bank + 4 < N_PAIRS:
-                    standardise(bank + 4)
+                if bank in (1, 3):
+                    standardise(2 + bank // 2)
                 if bank + 3 < N_PAIRS:
                     turn(bank + 3)
                 convolve(bank)
@@ -376,153 +400,141 @@ def tile_slstmblock_pa_kernel(
                     gain_and_bias(bank + 3)
                 silu(bank)
                 if 2 <= bank < 2 + NH:
-                    transpose_m(bank - 2)
+                    spread_biases(bank - 2)
                 if bank == BANKS - 2:
                     sum_biases()
             quantise_x_conv(NH - 1)
 
-        work = stack.enter_context(tc.tile_pool(name="work", bufs=3))
+        work = stack.enter_context(tc.tile_pool(name="work", bufs=2))
         stage = stack.enter_context(tc.tile_pool(name="stage", bufs=2))
-        gates = {}
-        parts = {}
-        backs = {}
+        pre_zo = {}
+        zo = {}
+        zo_back = {}
+        pre_if = {}
+        part = {}
         heads_out = {}
 
-        def gate_matmuls(out, r, gate, in_name):
-            head = r // TPH
-            cols = slice((r % TPH) * P, (r % TPH + 1) * P)
+        def gate_sum(out, head, gate, in_name, cols, rows, weights_stationary):
             for kind, name in (("in", in_name), ("rec", "h")):
                 codes, scales = w_mx[head * WPH + weight_list.index((kind, gate))]
+                w_op = (codes[:, cols].bitcast(FP8X4), scales[:, cols])
+                a_op = (act_codes[name][:, head, rows].bitcast(FP8X4), act_scales[name][:, head, rows])
+                left, right = (w_op, a_op) if weights_stationary else (a_op, w_op)
                 nc.tensor.matmul_mx(
-                    out=out,
-                    lhsT=codes[:, cols].bitcast(FP8X4), lhsT_scale=scales[:, cols],
-                    rhs=act_codes[name][:, head, :].bitcast(FP8X4), rhs_scale=act_scales[name][:, head, :],
+                    out=out, lhsT=left[0], lhsT_scale=left[1], rhs=right[0], rhs_scale=right[1],
                     start=(kind == "in"), stop=(kind == "rec"),
                 )
 
-        def matmuls(r):
-            zo = psum.tile([P, 2, B], F32, tag="m_zo", bufs=1)
-            gate_matmuls(zo[:, 0, :], r, GZ, "x")
-            gate_matmuls(zo[:, 1, :], r, GO, "x")
-            i_f = psum.tile([P, 2, B], F32, tag="words_if")
-            gate_matmuls(i_f[:, 0, :], r, GI, "c")
-            gate_matmuls(i_f[:, 1, :], r, GF, "c")
-            gates[r] = (zo, i_f)
-
-        def add_m_prev(r):
-            f_m = work.tile([P, B], F32)
-            nc.vector.scalar_tensor_tensor(
-                out=f_m[:], in0=gates[r][1][:, 1, :], scalar=gate_bias[:, GF, r:r + 1], in1=m_prev_t[:, r, :],
-                op0=ALU.add, op1=ALU.add,
-            )
-            parts[r] = {"f_m": f_m}
-
-        def difference(r):
-            d = work.tile([P, B], F32)
-            nc.vector.scalar_tensor_tensor(
-                out=d[:], in0=gates[r][1][:, 0, :], scalar=gate_bias[:, GI, r:r + 1], in1=parts[r]["f_m"][:],
-                op0=ALU.add, op1=ALU.subtract,
-            )
-            parts[r]["d"] = d
-
-        def drop_of(r):
-            drop = work.tile([P, B], F32)
-            nc.vector.tensor_scalar(
-                out=drop[:], in0=parts[r]["d"][:], scalar1=-1.0, scalar2=0.0, op0=ALU.mult, op1=ALU.max,
-            )
-            parts[r]["drop"] = drop
+        def sum_zo(r):
+            cols = slice((r % TPH) * P, (r % TPH + 1) * P)
+            sums = psum.tile([P, 2, B], F32, tag="words_zo")
+            for v, gate in enumerate((GZ, GO)):
+                gate_sum(sums[:, v, :], r // TPH, gate, "x", cols, slice(0, B), True)
+            pre_zo[r] = sums
 
         def squash(r):
-            zo = gates[r][0]
-            z = work.tile([P, B], F32)
-            nc.scalar.activation(out=z[:], in_=zo[:, 0, :], func=ACT.Tanh, bias=gate_bias[:, GZ, r:r + 1])
-            tanh_o = work.tile([P, B], F32)
-            nc.scalar.activation(
-                out=tanh_o[:], in_=zo[:, 1, :], func=ACT.Tanh, bias=half_o_bias[:, r:r + 1], scale=0.5,
-            )
-            parts[r]["z"] = z
-            parts[r]["tanh_o"] = tanh_o
+            z_o = work.tile([P, 2, B], F32, bufs=8)
+            for v, scale in enumerate((1.0, 0.5)):
+                nc.scalar.activation(
+                    out=z_o[:, v, :], in_=pre_zo[r][:, v, :], func=ACT.Tanh, bias=zo_bias[:, v, r:r + 1], scale=scale,
+                )
+            zo[r] = z_o
 
-        def exponentials(r):
-            part = parts[r]
-            fg = work.tile([P, B], F32)
-            nc.scalar.activation(out=fg[:], in_=part["d"][:], func=ACT.Exp, scale=-1.0)
-            ig = work.tile([P, B], F32)
-            nc.scalar.activation(out=ig[:], in_=part["drop"][:], func=ACT.Exp, scale=-1.0)
-            ig_z = work.tile([P, B], F32)
-            nc.gpsimd.tensor_tensor(out=ig_z[:], in0=ig[:], in1=part["z"][:], op=ALU.mult)
-            part["fg"], part["ig"], part["ig_z"] = fg, ig, ig_z
-
-        def transpose_back(r):
-            back_mul = psum.tile([P, 2, BT, P], F32, tag="conv_mul")
-            back_add = psum.tile([P, 2, BT, P], F32, tag="norm_add")
-            if r % 2 == 0:
-                back_m = psum.tile([P, 2, BT, P], F32, tag="m_m", bufs=1)
-            else:
-                back_m = backs[r - 1][2]
-            part = parts[r]
-
-            def back(out, names, t):
-                for v, name in enumerate(names):
-                    nc.tensor.matmul(
-                        out=out, lhsT=part[name][:, t * P:(t + 1) * P], rhs=ident_f32[:], is_transpose=True,
-                        start=(v == 0), stop=(v == len(names) - 1),
-                    )
-
+        def transpose_zo(head):
             for t in range(BT):
-                back(back_m[:, r % 2, t, :], ("f_m", "d", "drop"), t)
-            for t in range(BT):
-                back(back_mul[:, 0, t, :], ("fg",), t)
-                back(back_mul[:, 1, t, :], ("tanh_o",), t)
-            for t in range(BT):
-                back(back_add[:, 1, t, :], ("ig",), t)
-                back(back_add[:, 0, t, :], ("ig_z",), t)
-            backs[r] = (back_add, back_mul, back_m)
+                z_back = psum.tile([P, DH], F32, tag="conv_z")
+                o_back = psum.tile([P, DH], F32, tag="norm_o")
+                zo_back[head * BT + t] = (z_back, o_back)
+            for j in range(TPH):
+                for t in range(BT):
+                    for v in range(2):
+                        nc.tensor.transpose(
+                            out=zo_back[head * BT + t][v][:, j * P:(j + 1) * P],
+                            in_=zo[head * TPH + j][:, v, t * P:(t + 1) * P], identity=ident_f32[:],
+                        )
 
-        def keep_states(r):
-            if r % TPH == 0:
-                cn_new = stage.tile([P, 2, BT, DH], F32, bufs=NH)
+        def sum_if(u):
+            head, rows = u // BT, slice((u % BT) * P, (u % BT + 1) * P)
+            i_sum = psum.tile([P, DH], F32, tag="vec_i", bufs=1)
+            gate_sum(i_sum[:], head, GI, "c", slice(0, DH), rows, False)
+            f_sum = psum.tile([P, DH], F32, tag="vec_f", bufs=1)
+            gate_sum(f_sum[:], head, GF, "c", slice(0, DH), rows, False)
+            pre_if[u] = (i_sum, f_sum)
+
+        def shift_f(u):
+            head, t = u // BT, u % BT
+            if t == 0:
+                c_new = stage.tile([P, BT, DH], F32)
+                n_new = stage.tile([P, BT, DH], F32, bufs=NH)
                 oc_new = stage.tile([P, BT, DH], F32, bufs=NH)
                 m_new = stage.tile([P, BT, DH], F32)
-                heads_out[r // TPH] = {"cn": cn_new, "oc": oc_new, "m": m_new}
-            kept = work.tile([P, 2, BT, P], F32, bufs=2)
-            nc.vector.scalar_tensor_tensor(
-                out=kept[:], in0=backs[r][1][:, 0:1, :, :].to_broadcast([P, 2, BT, P]), scalar=1.0,
-                in1=cn_prev[:, :, :, r * P:(r + 1) * P], op0=ALU.min, op1=ALU.mult,
-            )
-            parts[r]["kept"] = kept
+                heads_out[head] = {"c": c_new, "n": n_new, "oc": oc_new, "m": m_new}
+            f_s = m_shift[:, t, head * DH:(head + 1) * DH]
+            nc.vector.tensor_tensor(out=f_s, in0=pre_if[u][1][:], in1=f_s, op=ALU.add)
+            part[u] = {"f_s": f_s}
 
-        def add_inputs(r):
-            cols = slice((r % TPH) * P, (r % TPH + 1) * P)
+        def difference(u):
+            d = work.tile([P, DH], F32)
+            nc.vector.tensor_tensor(out=d[:], in0=pre_if[u][0][:], in1=part[u]["f_s"], op=ALU.subtract)
+            part[u]["d"] = d
+
+        def stabilise(u):
+            head, t = u // BT, u % BT
+            m_t = heads_out[head]["m"][:, t, :]
+            nc.vector.scalar_tensor_tensor(
+                out=m_t, in0=part[u]["d"][:], scalar=0.0, in1=part[u]["f_s"], op0=ALU.max, op1=ALU.add,
+            )
+            nc.gpsimd.tensor_tensor(out=m_t, in0=m_t, in1=i_bias[:, head * DH:(head + 1) * DH], op=ALU.add)
+
+        def exponentials(u):
+            fg = work.tile([P, 1, DH], F32)
+            nc.scalar.activation(out=fg[:, 0, :], in_=part[u]["d"][:], func=ACT.Exp, scale=-1.0)
+            ig = work.tile([P, DH], F32)
+            nc.scalar.activation(out=ig[:], in_=part[u]["d"][:], func=ACT.Exp)
+            part[u]["fg"], part[u]["ig"] = fg, ig
+
+        def keep_states(u):
+            head, t = u // BT, u % BT
+            kept = work.tile([P, 2, DH], F32)
+            nc.vector.scalar_tensor_tensor(
+                out=kept[:], in0=part[u]["fg"][:].to_broadcast([P, 2, DH]), scalar=1.0,
+                in1=cn_prev[:, :, t, head * DH:(head + 1) * DH], op0=ALU.min, op1=ALU.mult,
+            )
+            part[u]["kept"] = kept
+
+        def input_term(u):
+            ig_z = work.tile([P, DH], F32)
+            nc.vector.scalar_tensor_tensor(
+                out=ig_z[:], in0=part[u]["ig"][:], scalar=1.0, in1=zo_back[u][0][:], op0=ALU.min, op1=ALU.mult,
+            )
+            part[u]["ig_z"] = ig_z
+
+        def new_n(u):
+            nc.vector.scalar_tensor_tensor(
+                out=heads_out[u // BT]["n"][:, u % BT, :], in0=part[u]["ig"][:], scalar=1.0, in1=part[u]["kept"][:, 1, :],
+                op0=ALU.min, op1=ALU.add,
+            )
+
+        def new_c(u):
             nc.vector.tensor_tensor(
-                out=heads_out[r // TPH]["cn"][:, :, :, cols], in0=parts[r]["kept"][:], in1=backs[r][0][:], op=ALU.add,
+                out=heads_out[u // BT]["c"][:, u % BT, :], in0=part[u]["kept"][:, 0, :], in1=part[u]["ig_z"][:], op=ALU.add,
             )
 
-        def open_output(r):
-            outs = heads_out[r // TPH]
-            cols = slice((r % TPH) * P, (r % TPH + 1) * P)
+        def open_output(u):
+            outs = heads_out[u // BT]
             nc.vector.scalar_tensor_tensor(
-                out=outs["oc"][:, :, cols], in0=backs[r][1][:, 1, :, :], scalar=1.0, in1=outs["cn"][:, 0, :, cols],
+                out=outs["oc"][:, u % BT, :], in0=zo_back[u][1][:], scalar=1.0, in1=outs["c"][:, u % BT, :],
                 op0=ALU.add, op1=ALU.mult,
             )
 
-        def copy_m(r):
-            cols = slice((r % TPH - 1) * P, (r % TPH + 1) * P)
-            (nc.vector.tensor_copy if r == NT - 1 else nc.scalar.copy)(
-                out=heads_out[r // TPH]["m"][:, :, cols].rearrange("p t (q c) -> p t q c", q=2),
-                in_=backs[r][2][:].rearrange("p q t c -> p t q c"),
-            )
-
         def store_states(head):
-            outs = heads_out[head]
             hcols = slice(head * DH, (head + 1) * DH)
-            nc.sync.dma_start(out=batch_tiles(out_m)[:, :, hcols], in_=outs["m"][:])
-            nc.sync.dma_start(out=batch_tiles(out_c)[:, :, hcols], in_=outs["cn"][:, 0, :, :])
-            nc.sync.dma_start(out=batch_tiles(out_n)[:, :, hcols], in_=outs["cn"][:, 1, :, :])
+            for name, dst in (("c", out_c), ("n", out_n), ("m", out_m)):
+                nc.sync.dma_start(out=batch_tiles(dst)[:, :, hcols], in_=heads_out[head][name][:])
 
         def log_of_n(head):
             outs = heads_out[head]
-            n_new = outs["cn"][:, 1, :, :]
+            n_new = outs["n"][:]
             if head == NH - 1:
                 last_log = stage.tile([P, BT, DH], F32, bufs=1)
                 outs["log"] = last_log[:]
@@ -537,36 +549,43 @@ def tile_slstmblock_pa_kernel(
             hcols = slice(head * DH, (head + 1) * DH)
             nc.sync.dma_start(out=batch_tiles(out_h)[:, :, hcols], in_=outs["oc"][:])
 
-        matmuls(0)
-        for r in range(NT + BACK_LAG):
-            back = r - BACK_LAG
-            if r == NT:
-                for head in range(NH - 1):
-                    log_of_n(head)
-            if r < NT:
-                add_m_prev(r)
+        for r in range(TPH):
+            sum_zo(r)
+            squash(r)
+        transpose_zo(0)
+        sum_if(0)
+        for u in range(STEPS + 1):
+            head, t, back = u // BT, u % BT, u - 1
+            if u == STEPS:
+                for done in range(NH - 1):
+                    log_of_n(done)
+            if u < STEPS:
+                shift_f(u)
             if back >= 0:
                 keep_states(back)
-            if r < NT:
-                difference(r)
-                squash(r)
+            if u < STEPS:
+                difference(u)
+            take_weights(17 + QUANT_LAG + 3 * u)
             if back >= 0:
-                add_inputs(back)
-            if r < NT:
-                drop_of(r)
+                input_term(back)
+                new_n(back)
+            if u < STEPS:
+                stabilise(u)
+                exponentials(u)
+            if back >= 0:
+                new_c(back)
+            if u + 1 < STEPS:
+                sum_if(u + 1)
+            if t == 1 and head + 1 < NH:
+                for j in range(TPH):
+                    sum_zo((head + 1) * TPH + j)
+                    squash((head + 1) * TPH + j)
             if back >= 0:
                 open_output(back)
-            if r + 1 < NT:
-                matmuls(r + 1)
-            take_weights(16 + 2 * r)
-            if r < NT:
-                exponentials(r)
-            if back >= 0 and back % 2 == 1:
-                copy_m(back)
-            if 0 <= r - BACK_LAG + 1 < NT:
-                transpose_back(r - BACK_LAG + 1)
-            if back >= 0 and back % TPH == TPH - 1:
-                store_states(back // TPH)
+                if t == 0:
+                    store_states(head - 1)
+                    if head < NH:
+                        transpose_zo(head)
         log_of_n(NH - 1)
         for head in range(NH):
             finish_h(head)

@@ -31,6 +31,8 @@ RAW_BUFS = 6
 N_PAIRS = NT // 2
 BANKS = NH * BT
 QUANT_LAG = 2
+EARLY_HEADS = 2
+EARLY_STEP = 6
 STEPS = NH * BT
 
 FLOPS = 8 * 2 * B * D * DH
@@ -532,22 +534,24 @@ def tile_slstmblock_pa_kernel(
             for name, dst in (("c", out_c), ("n", out_n), ("m", out_m)):
                 nc.sync.dma_start(out=batch_tiles(dst)[:, :, hcols], in_=heads_out[head][name][:])
 
-        def log_of_n(head):
+        def log_of_n(head, rows=slice(0, BT)):
             outs = heads_out[head]
-            n_new = outs["n"][:]
-            if head == NH - 1:
+            if head < NH - 1:
+                outs["log"] = outs["n"]
+            elif rows.start == 0:
                 last_log = stage.tile([P, BT, DH], F32, bufs=1)
-                outs["log"] = last_log[:]
-            else:
-                outs["log"] = n_new
-            nc.scalar.activation(out=outs["log"], in_=n_new, func=ACT.Ln, scale=2.0, bias=two_eps[:, 0:1])
+                outs["log"] = last_log
+            nc.scalar.activation(
+                out=outs["log"][:, rows, :], in_=outs["n"][:, rows, :], func=ACT.Ln, scale=2.0, bias=two_eps[:, 0:1],
+            )
 
-        def finish_h(head):
+        def finish_h(head, rows=slice(0, BT)):
             outs = heads_out[head]
-            nc.scalar.activation(out=outs["log"], in_=outs["log"], func=ACT.Exp, scale=-1.0)
-            nc.vector.tensor_tensor(out=outs["oc"][:], in0=outs["oc"][:], in1=outs["log"], op=ALU.mult)
+            log, h_new = outs["log"][:, rows, :], outs["oc"][:, rows, :]
+            nc.scalar.activation(out=log, in_=log, func=ACT.Exp, scale=-1.0)
+            nc.vector.tensor_tensor(out=h_new, in0=h_new, in1=log, op=ALU.mult)
             hcols = slice(head * DH, (head + 1) * DH)
-            nc.sync.dma_start(out=batch_tiles(out_h)[:, :, hcols], in_=outs["oc"][:])
+            nc.sync.dma_start(out=batch_tiles(out_h)[:, rows, hcols], in_=h_new)
 
         for r in range(TPH):
             sum_zo(r)
@@ -556,8 +560,8 @@ def tile_slstmblock_pa_kernel(
         sum_if(0)
         for u in range(STEPS + 1):
             head, t, back = u // BT, u % BT, u - 1
-            if u == STEPS:
-                for done in range(NH - 1):
+            if u == EARLY_STEP:
+                for done in range(EARLY_HEADS):
                     log_of_n(done)
             if u < STEPS:
                 shift_f(u)
@@ -586,6 +590,13 @@ def tile_slstmblock_pa_kernel(
                     store_states(head - 1)
                     if head < NH:
                         transpose_zo(head)
-        log_of_n(NH - 1)
-        for head in range(NH):
+        for head in range(EARLY_HEADS):
             finish_h(head)
+        for head in range(EARLY_HEADS, NH - 1):
+            log_of_n(head)
+        for t in range(BT):
+            log_of_n(NH - 1, slice(t, t + 1))
+        for head in range(EARLY_HEADS, NH - 1):
+            finish_h(head)
+        for t in range(BT):
+            finish_h(NH - 1, slice(t, t + 1))

@@ -111,14 +111,14 @@ def tile_slstmblock_pa_kernel(
                 load_weight(w, raw)
 
         def on_vector(w):
-            return w not in (1, 3, 5, 7, 9) if w < 2 * WPH else w % WPH in (0, 2, 4)
+            return w not in (1, 3, 5, 7, 9, 13) if w < 2 * WPH else w % WPH in (0, 2, 4)
 
         def regroup_weight(w):
             grouped = w_grp_pool.tile(
                 [P, DH, PACK], BF16, align_bytes=64, tag="vector" if on_vector(w) else "scalar",
             )
-            dst = grouped[:].rearrange("p (c i) t -> p c t i", i=4)
-            src = w_raw[w][:].rearrange("p t (c i) -> p c t i", i=4)
+            dst = grouped[:].rearrange("p (c i) t -> p c t i", i=8)
+            src = w_raw[w][:].rearrange("p t (c i) -> p c t i", i=8)
             if on_vector(w):
                 nc.vector.tensor_copy(out=dst, in_=src)
             else:

from contextlib import ExitStack

import concourse.mybir as mybir
from concourse.masks import make_identity

F32 = mybir.dt.float32
BF16 = mybir.dt.bfloat16
U32 = mybir.dt.uint32
U8 = mybir.dt.uint8
FP8X4 = mybir.dt.float8_e4m3fn_x4
ACT = mybir.ActivationFunctionType
ALU = mybir.AluOpType

P = 128
B = 256
BT = B // P
D = 2048
NH = 4
DH = D // NH
PACK = 4
NT = D // P
TPH = DH // P
KC = 4
LN_EPS = 1e-5
H_EPS = 1e-6
GZ, GI, GF, GO = 0, 1, 2, 3
WPH = 8
N_WEIGHTS = WPH * NH
RAW_FIRST = 6
RAW_BUFS = 6
N_PAIRS = NT // 2
BANKS = NH * BT
QUANT_LAG = 2
EARLY_HEADS = 2
EARLY_STEP = 6
STEPS = NH * BT

FLOPS = 8 * 2 * B * D * DH


def batch_tiles(ap):
    return ap.rearrange("(t p) d -> p t d", p=P)


def tile_slstmblock_pa_kernel(
    tc,
    x, h_prev, c_prev, n_prev, m_prev, ln_g, ln_b, conv_w, conv_b,
    wz_w, wz_b, wi_w, wi_b, wf_w, wf_b, wo_w, wo_b,
    rz_w, rz_b, ri_w, ri_b, rf_w, rf_b, ro_w, ro_b,
    out_h, out_c, out_n, out_m,
):
    nc = tc.nc
    in_weights = (wz_w, wi_w, wf_w, wo_w)
    rec_weights = (rz_w, ri_w, rf_w, ro_w)

    with ExitStack() as stack:
        keep = stack.enter_context(tc.tile_pool(name="keep", bufs=1))
        w_raw_pool = stack.enter_context(tc.tile_pool(name="w_raw", bufs=RAW_BUFS))
        w_grp_pool = stack.enter_context(tc.tile_pool(name="w_grp", bufs=3))
        w_mx_pool = stack.enter_context(tc.tile_pool(name="w_mx", bufs=2))
        psum = stack.enter_context(tc.psum_pool(name="psum", bufs=2))

        stack.enter_context(tc.manual_schedule(engines={mybir.EngineType.Activation}))

        ident_f32 = keep.tile([P, P], F32)
        make_identity(nc, ident_f32[:])
        ident_bf = keep.tile([P, P], BF16)
        make_identity(nc, ident_bf[:])
        minus_half = keep.tile([P, 1], F32)
        nc.vector.memset(minus_half[:], -0.5)
        two_eps = keep.tile([P, 1], F32)
        nc.vector.memset(two_eps[:], 2.0 * H_EPS)

        table_warm = keep.tile([P, 1], F32)
        nc.scalar.activation(out=table_warm[:], in_=two_eps[:], func=ACT.Silu)

        act_codes = {}
        act_scales = {}
        for name in ("x", "h", "c"):
            act_codes[name] = keep.tile([P, NH, B], U32, name="codes_" + name, align_bytes=64)
            act_scales[name] = keep.tile([P, NH, B], U8, name="scales_" + name, align_bytes=64)

        m_shift = keep.tile([P, BT, D], F32)
        i_bias = keep.tile([P, D], F32)
        cn_prev = keep.tile([P, 2, BT, D], BF16)
        zo_bias = keep.tile([P, 2, NT], F32)

        weight_list = []
        for gate in (GZ, GO, GI, GF):
            weight_list.append(("in", gate))
            weight_list.append(("rec", gate))
        w_raw = {}
        w_grouped = {}
        w_mx = {}

        def load_weight(w, raw):
            kind, gate = weight_list[w % WPH]
            w_head = (in_weights[gate] if kind == "in" else rec_weights[gate])[w // WPH]
            if kind == "in" and gate in (GI, GF):
                nc.sync.dma_start(out=raw[:], in_=w_head.rearrange("(t p) n -> p t n", p=P))
            else:
                nc.sync.dma_start(
                    out=raw[:].rearrange("q (u e) n -> q u (e n)", u=2),
                    in_=w_head.rearrange("(u q e) n -> q u (e n)", u=2, e=2),
                )
            w_raw[w] = raw

        def load_ring(w):
            if w < N_WEIGHTS:
                raw = w_raw_pool.tile([P, PACK, DH], BF16)
                load_weight(w, raw)

        def on_vector(w):
            return w not in (1, 3, 5, 7, 9, 13) if w < 2 * WPH else w % WPH in (0, 2, 4)

        def regroup_weight(w):
            grouped = w_grp_pool.tile(
                [P, DH, PACK], BF16, align_bytes=64, tag="vector" if on_vector(w) else "scalar",
            )
            dst = grouped[:].rearrange("p (c i) t -> p c t i", i=8)
            src = w_raw[w][:].rearrange("p t (c i) -> p c t i", i=8)
            if on_vector(w):
                nc.vector.tensor_copy(out=dst, in_=src)
            else:
                nc.scalar.copy(out=dst, in_=src)
            w_grouped[w] = grouped
            if w >= RAW_FIRST:
                load_ring(w + RAW_BUFS)

        def quantise_weight(w):
            codes = w_mx_pool.tile([P, DH], U32, tag="codes%d" % (w % WPH), align_bytes=64)
            scales = w_mx_pool.tile([P, DH], U8, tag="scales%d" % (w % WPH), align_bytes=64)
            nc.vector.quantize_mx(
                out=codes[:].bitcast(FP8X4),
                scales=scales[:],
                in_=w_grouped[w][:].rearrange("p n t -> p (n t)"),
            )
            w_mx[w] = (codes, scales)

        taken = []

        def take_weights(upto):
            for w in range(len(taken), min(upto, N_WEIGHTS + QUANT_LAG)):
                taken.append(w)
                if w < N_WEIGHTS:
                    regroup_weight(w)
                if w >= QUANT_LAG:
                    quantise_weight(w - QUANT_LAG)

        with tc.tile_pool(name="pro", bufs=1) as pro:
            x_sb = pro.tile([P, BT, D], BF16)
            h_sb = pro.tile([P, BT, D], BF16)
            m_sb = pro.tile([P, BT, D], BF16)

            def load_first(w):
                raw = pro.tile([P, PACK, DH], BF16, tag="raw_first", bufs=RAW_FIRST)
                load_weight(w, raw)

            bias_rows = pro.tile([P, P], BF16)
            ln_rows = pro.tile([P, P], BF16)
            nc.vector.memset(ln_rows[:], 0.0)
            taps_bf = pro.tile([P, KC], BF16)
            conv_bias_bf = pro.tile([P, 1], BF16)
            with nc.allow_non_contiguous_dma(reason="small vectors"):
                nc.sync.dma_start(out=taps_bf[:], in_=conv_w.partition_broadcast(P))
                nc.sync.dma_start(out=conv_bias_bf[:], in_=conv_b.partition_broadcast(P))
                for t in range(BT):
                    nc.sync.dma_start(out=x_sb[:, t, :], in_=x[t * P:(t + 1) * P, :])
                for v, vec in enumerate((ln_g, ln_b)):
                    nc.sync.dma_start(out=ln_rows[NT * v:NT * (v + 1), :], in_=vec.rearrange("(r c) -> r c", c=P))
            for w in range(4):
                load_first(w)
            with nc.allow_non_contiguous_dma(reason="small vectors"):
                for v, vec in enumerate((wz_b, wi_b, wf_b, wo_b, rz_b, ri_b, rf_b, ro_b)):
                    nc.sync.dma_start(out=bias_rows[NT * v:NT * (v + 1), :], in_=vec.rearrange("(r c) -> r c", c=P))
            nc.sync.dma_start(out=h_sb[:], in_=batch_tiles(h_prev))
            for w in range(4, RAW_FIRST):
                load_first(w)
            nc.sync.dma_start(out=m_sb[:], in_=batch_tiles(m_prev))
            for w in range(RAW_FIRST, RAW_FIRST + RAW_BUFS):
                load_ring(w)
            nc.sync.dma_start(out=cn_prev[:, 0, :, :], in_=batch_tiles(c_prev))
            nc.sync.dma_start(out=cn_prev[:, 1, :, :], in_=batch_tiles(n_prev))

            taps = pro.tile([P, KC], F32)
            nc.vector.tensor_copy(out=taps[:], in_=taps_bf[:])
            conv_bias = pro.tile([P, 1], F32)
            nc.vector.tensor_copy(out=conv_bias[:], in_=conv_bias_bf[:])
            band = pro.tile([P, 2 * P], F32)
            nc.vector.memset(band[:], 0.0)
            for s in range(KC):
                nc.vector.scalar_tensor_tensor(
                    out=band[:, s:s + P], in0=ident_f32[:], scalar=taps[:, KC - 1 - s:KC - s],
                    in1=band[:, s:s + P], op0=ALU.mult, op1=ALU.add,
                )
            stats = pro.tile([P, BT, NH, 6], F32)
            mean_var = pro.tile([P, BT, 2], F32)
            var_eps = pro.tile([P, BT], F32)
            rstd = pro.tile([P, BT], F32)
            shift = pro.tile([P, BT], F32)

            def statistics():
                for t in range(BT):
                    for head in range(NH):
                        nc.vector.bn_stats(out=stats[:, t, head, :], in_=x_sb[:, t, head * DH:(head + 1) * DH])
                    nc.vector.bn_aggr(out=mean_var[:, t, :], in_=stats[:, t, :, :].rearrange("p c s -> p (c s)"))
                    nc.vector.tensor_scalar_add(out=var_eps[:, t:t + 1], in0=mean_var[:, t, 1:2], scalar1=LN_EPS)
                    nc.gpsimd.tensor_tensor(out=rstd[:, t:t + 1], in0=var_eps[:, t:t + 1], in1=minus_half[:], op=ALU.pow)

            ln_cols = pro.tile([P, 2, NT], F32)

            def gain_and_bias_columns():
                ln_ps = psum.tile([P, P], BF16, tag="vec_i", bufs=1)
                nc.tensor.transpose(out=ln_ps[:], in_=ln_rows[:], identity=ident_bf[:])
                nc.vector.tensor_copy(out=ln_cols[:].rearrange("p v r -> p (v r)"), in_=ln_ps[:, 0:2 * NT])

            def finish_statistics():
                for t in range(BT):
                    nc.vector.scalar_tensor_tensor(
                        out=shift[:, t:t + 1], in0=mean_var[:, t, 0:1], scalar=-1.0, in1=rstd[:, t:t + 1],
                        op0=ALU.mult, op1=ALU.mult,
                    )

            x_norm_t = {}

            x_hat = {}

            def standardise(head):
                hat = pro.tile([P, BT, DH], F32, bufs=3)
                for t in range(BT):
                    nc.vector.tensor_scalar(
                        out=hat[:, t, :], in0=x_sb[:, t, head * DH:(head + 1) * DH],
                        scalar1=rstd[:, t:t + 1], scalar2=shift[:, t:t + 1], op0=ALU.mult, op1=ALU.add,
                    )
                for half in range(2):
                    x_hat[2 * head + half] = hat[:, :, half * 2 * P:(half + 1) * 2 * P]

            x_hat_t = {}

            def turn(pair):
                hat_t = psum.tile([P, 2, B], F32, tag="norm_o")
                for i in range(2):
                    for t in range(BT):
                        nc.tensor.transpose(
                            out=hat_t[:, i, t * P:(t + 1) * P], in_=x_hat[pair][:, t, i * P:(i + 1) * P],
                            identity=ident_f32[:],
                        )
                x_hat_t[pair] = hat_t

            def gain_and_bias(pair):
                x_norm = pro.tile([P, 2, B], F32, bufs=N_PAIRS)
                for i in range(2):
                    r = 2 * pair + i
                    nc.scalar.activation(
                        out=x_norm[:, i, :], in_=x_hat_t[pair][:, i, :], func=ACT.Identity,
                        scale=ln_cols[:, 0, r:r + 1], bias=ln_cols[:, 1, r:r + 1],
                    )
                x_norm_t[pair] = x_norm

            c_grouped = {}
            conv_out = {}

            def convolve(bank):
                head, t = bank // BT, bank % BT
                if t == 0:
                    grouped = pro.tile([P, B, PACK], BF16, align_bytes=64, bufs=2, name="c_grouped")
                    c_grouped[head] = grouped
                rows = slice(t * P, (t + 1) * P)
                conv_t = psum.tile([P, TPH, P], F32, tag="conv_z")
                for j in range(TPH):
                    r = head * TPH + j
                    nc.tensor.matmul(
                        out=conv_t[:, j, :], lhsT=band[:, 0:P], rhs=x_norm_t[r // 2][:, r % 2, rows],
                        start=True, stop=(r == 0),
                    )
                    if r > 0:
                        nc.tensor.matmul(
                            out=conv_t[:, j, :], lhsT=band[:, P:2 * P],
                            rhs=x_norm_t[(r - 1) // 2][:, (r - 1) % 2, rows],
                            start=False, stop=True,
                        )
                conv_out[bank] = conv_t

            def silu(bank):
                head, t = bank // BT, bank % BT
                nc.scalar.activation(
                    out=c_grouped[head][:, t * P:(t + 1) * P, :], in_=conv_out[bank][:].rearrange("p j b -> p b j"),
                    func=ACT.Silu, bias=conv_bias[:, 0:1],
                )

            def quantise_x_conv(head):
                nc.vector.quantize_mx(
                    out=act_codes["c"][:, head, :].bitcast(FP8X4),
                    scales=act_scales["c"][:, head, :],
                    in_=c_grouped[head][:].rearrange("p b t -> p (b t)"),
                )

            words = {}

            def transpose_words(src, name, head):
                grouped = pro.tile([P, B, PACK], BF16, align_bytes=64, bufs=4)
                words_t = psum.tile([P, 2, B], F32, tag="words_zo")
                for u in range(2):
                    for t in range(BT):
                        first = head * (DH // 2) + u * P
                        nc.tensor.transpose(
                            out=words_t[:, u, t * P:(t + 1) * P],
                            in_=src[:, t, :].bitcast(F32)[:, first:first + P],
                            identity=ident_f32[:],
                        )
                nc.scalar.copy(
                    out=grouped[:].bitcast(F32),
                    in_=words_t[:].rearrange("p u b -> p b u"),
                )
                words[name, head] = grouped

            def quantise_words(name, head):
                nc.vector.quantize_mx(
                    out=act_codes[name][:, head, :].bitcast(FP8X4),
                    scales=act_scales[name][:, head, :],
                    in_=words[name, head][:].rearrange("p b t -> p (b t)"),
                )

            selector = pro.tile([P, 2, NT], BF16)

            def make_selector():
                f_rows = pro.tile([P, NT], BF16)
                nc.vector.tensor_tensor(
                    out=selector[:, 1, :], in0=ident_bf[:, GI * NT:(GI + 1) * NT],
                    in1=ident_bf[:, (4 + GI) * NT:(5 + GI) * NT], op=ALU.add,
                )
                nc.vector.tensor_tensor(
                    out=f_rows[:], in0=ident_bf[:, GF * NT:(GF + 1) * NT],
                    in1=ident_bf[:, (4 + GF) * NT:(5 + GF) * NT], op=ALU.add,
                )
                nc.vector.tensor_tensor(out=selector[:, 0, :], in0=f_rows[:], in1=selector[:, 1, :], op=ALU.subtract)

            def spread_biases(head):
                hcols = slice(head * DH, (head + 1) * DH)
                spread = []
                for v, tag in enumerate(("vec_i", "vec_f")):
                    rows = psum.tile([P, DH], F32, tag=tag, bufs=1, name="spread")
                    for j in range(TPH):
                        r = head * TPH + j
                        nc.tensor.matmul(
                            out=rows[:, j * P:(j + 1) * P], lhsT=selector[:, v, r:r + 1].to_broadcast([P, P]),
                            rhs=bias_rows[:], start=True, stop=True,
                        )
                    spread.append(rows)
                nc.vector.tensor_tensor(
                    out=m_shift[:, :, hcols], in0=m_sb[:, :, hcols],
                    in1=spread[0][:].unsqueeze(1).to_broadcast([P, BT, DH]), op=ALU.add,
                )
                nc.scalar.copy(out=i_bias[:, hcols], in_=spread[1][:])

            def sum_biases():
                bias_ps = psum.tile([P, P], BF16, tag="norm_o")
                nc.tensor.transpose(out=bias_ps[:], in_=bias_rows[:], identity=ident_bf[:])
                bias_cols = pro.tile([P, P], F32)
                nc.vector.tensor_copy(out=bias_cols[:], in_=bias_ps[:])
                o_sum = pro.tile([P, NT], F32)
                for out, gate in ((zo_bias[:, 0, :], GZ), (o_sum[:], GO)):
                    nc.vector.tensor_tensor(
                        out=out, in0=bias_cols[:, gate * NT:(gate + 1) * NT],
                        in1=bias_cols[:, (4 + gate) * NT:(5 + gate) * NT], op=ALU.add,
                    )
                nc.vector.tensor_scalar_mul(out=zo_bias[:, 1, :], in0=o_sum[:], scalar1=0.5)

            make_selector()
            statistics()
            for head in range(NH):
                transpose_words(x_sb, "x", head)
            take_weights(1)
            gain_and_bias_columns()
            finish_statistics()
            for head in range(2):
                standardise(head)
            for head in range(NH):
                quantise_words("x", head)
            take_weights(4)
            turn(0)
            turn(1)
            gain_and_bias(0)
            gain_and_bias(1)
            for head in range(NH):
                transpose_words(h_sb, "h", head)
            take_weights(6)
            turn(2)
            gain_and_bias(2)
            for bank in range(BANKS):
                if bank in (1, 3):
                    standardise(2 + bank // 2)
                if bank + 3 < N_PAIRS:
                    turn(bank + 3)
                convolve(bank)
                take_weights(7 + bank + bank // 4)
                if bank < NH:
                    quantise_words("h", bank)
                if bank % 2 == 0 and bank > 0:
                    quantise_x_conv(bank // 2 - 1)
                if bank + 3 < N_PAIRS:
                    gain_and_bias(bank + 3)
                silu(bank)
                if 2 <= bank < 2 + NH:
                    spread_biases(bank - 2)
                if bank == BANKS - 2:
                    sum_biases()
            quantise_x_conv(NH - 1)

        work = stack.enter_context(tc.tile_pool(name="work", bufs=2))
        stage = stack.enter_context(tc.tile_pool(name="stage", bufs=2))
        pre_zo = {}
        zo = {}
        zo_back = {}
        pre_if = {}
        part = {}
        heads_out = {}

        def gate_sum(out, head, gate, in_name, cols, rows, weights_stationary):
            for kind, name in (("in", in_name), ("rec", "h")):
                codes, scales = w_mx[head * WPH + weight_list.index((kind, gate))]
                w_op = (codes[:, cols].bitcast(FP8X4), scales[:, cols])
                a_op = (act_codes[name][:, head, rows].bitcast(FP8X4), act_scales[name][:, head, rows])
                left, right = (w_op, a_op) if weights_stationary else (a_op, w_op)
                nc.tensor.matmul_mx(
                    out=out, lhsT=left[0], lhsT_scale=left[1], rhs=right[0], rhs_scale=right[1],
                    start=(kind == "in"), stop=(kind == "rec"),
                )

        def sum_zo(r):
            cols = slice((r % TPH) * P, (r % TPH + 1) * P)
            sums = psum.tile([P, 2, B], F32, tag="words_zo")
            for v, gate in enumerate((GZ, GO)):
                gate_sum(sums[:, v, :], r // TPH, gate, "x", cols, slice(0, B), True)
            pre_zo[r] = sums

        def squash(r):
            z_o = work.tile([P, 2, B], F32, bufs=8)
            for v, scale in enumerate((1.0, 0.5)):
                nc.scalar.activation(
                    out=z_o[:, v, :], in_=pre_zo[r][:, v, :], func=ACT.Tanh, bias=zo_bias[:, v, r:r + 1], scale=scale,
                )
            zo[r] = z_o

        def transpose_zo(head):
            for t in range(BT):
                z_back = psum.tile([P, DH], F32, tag="conv_z")
                o_back = psum.tile([P, DH], F32, tag="norm_o")
                zo_back[head * BT + t] = (z_back, o_back)
            for j in range(TPH):
                for t in range(BT):
                    for v in range(2):
                        nc.tensor.transpose(
                            out=zo_back[head * BT + t][v][:, j * P:(j + 1) * P],
                            in_=zo[head * TPH + j][:, v, t * P:(t + 1) * P], identity=ident_f32[:],
                        )

        def sum_if(u):
            head, rows = u // BT, slice((u % BT) * P, (u % BT + 1) * P)
            i_sum = psum.tile([P, DH], F32, tag="vec_i", bufs=1)
            gate_sum(i_sum[:], head, GI, "c", slice(0, DH), rows, False)
            f_sum = psum.tile([P, DH], F32, tag="vec_f", bufs=1)
            gate_sum(f_sum[:], head, GF, "c", slice(0, DH), rows, False)
            pre_if[u] = (i_sum, f_sum)

        def shift_f(u):
            head, t = u // BT, u % BT
            if t == 0:
                c_new = stage.tile([P, BT, DH], F32)
                n_new = stage.tile([P, BT, DH], F32, bufs=NH)
                oc_new = stage.tile([P, BT, DH], F32, bufs=NH)
                m_new = stage.tile([P, BT, DH], F32)
                heads_out[head] = {"c": c_new, "n": n_new, "oc": oc_new, "m": m_new}
            f_s = m_shift[:, t, head * DH:(head + 1) * DH]
            nc.vector.tensor_tensor(out=f_s, in0=pre_if[u][1][:], in1=f_s, op=ALU.add)
            part[u] = {"f_s": f_s}

        def difference(u):
            d = work.tile([P, DH], F32)
            nc.vector.tensor_tensor(out=d[:], in0=pre_if[u][0][:], in1=part[u]["f_s"], op=ALU.subtract)
            part[u]["d"] = d

        def stabilise(u):
            head, t = u // BT, u % BT
            m_t = heads_out[head]["m"][:, t, :]
            nc.vector.scalar_tensor_tensor(
                out=m_t, in0=part[u]["d"][:], scalar=0.0, in1=part[u]["f_s"], op0=ALU.max, op1=ALU.add,
            )
            nc.gpsimd.tensor_tensor(out=m_t, in0=m_t, in1=i_bias[:, head * DH:(head + 1) * DH], op=ALU.add)

        def exponentials(u):
            fg = work.tile([P, 1, DH], F32)
            nc.scalar.activation(out=fg[:, 0, :], in_=part[u]["d"][:], func=ACT.Exp, scale=-1.0)
            ig = work.tile([P, DH], F32)
            nc.scalar.activation(out=ig[:], in_=part[u]["d"][:], func=ACT.Exp)
            part[u]["fg"], part[u]["ig"] = fg, ig

        def keep_states(u):
            head, t = u // BT, u % BT
            kept = work.tile([P, 2, DH], F32)
            nc.vector.scalar_tensor_tensor(
                out=kept[:], in0=part[u]["fg"][:].to_broadcast([P, 2, DH]), scalar=1.0,
                in1=cn_prev[:, :, t, head * DH:(head + 1) * DH], op0=ALU.min, op1=ALU.mult,
            )
            part[u]["kept"] = kept

        def input_term(u):
            ig_z = work.tile([P, DH], F32)
            nc.vector.scalar_tensor_tensor(
                out=ig_z[:], in0=part[u]["ig"][:], scalar=1.0, in1=zo_back[u][0][:], op0=ALU.min, op1=ALU.mult,
            )
            part[u]["ig_z"] = ig_z

        def new_n(u):
            nc.vector.scalar_tensor_tensor(
                out=heads_out[u // BT]["n"][:, u % BT, :], in0=part[u]["ig"][:], scalar=1.0, in1=part[u]["kept"][:, 1, :],
                op0=ALU.min, op1=ALU.add,
            )

        def new_c(u):
            nc.vector.tensor_tensor(
                out=heads_out[u // BT]["c"][:, u % BT, :], in0=part[u]["kept"][:, 0, :], in1=part[u]["ig_z"][:], op=ALU.add,
            )

        def open_output(u):
            outs = heads_out[u // BT]
            nc.vector.scalar_tensor_tensor(
                out=outs["oc"][:, u % BT, :], in0=zo_back[u][1][:], scalar=1.0, in1=outs["c"][:, u % BT, :],
                op0=ALU.add, op1=ALU.mult,
            )

        def store_states(head):
            hcols = slice(head * DH, (head + 1) * DH)
            for name, dst in (("c", out_c), ("n", out_n), ("m", out_m)):
                nc.sync.dma_start(out=batch_tiles(dst)[:, :, hcols], in_=heads_out[head][name][:])

        def log_of_n(head, rows=slice(0, BT)):
            outs = heads_out[head]
            if head < NH - 1:
                outs["log"] = outs["n"]
            elif rows.start == 0:
                last_log = stage.tile([P, BT, DH], F32, bufs=1)
                outs["log"] = last_log
            nc.scalar.activation(
                out=outs["log"][:, rows, :], in_=outs["n"][:, rows, :], func=ACT.Ln, scale=2.0, bias=two_eps[:, 0:1],
            )

        def finish_h(head, rows=slice(0, BT)):
            outs = heads_out[head]
            log, h_new = outs["log"][:, rows, :], outs["oc"][:, rows, :]
            nc.scalar.activation(out=log, in_=log, func=ACT.Exp, scale=-1.0)
            nc.vector.tensor_tensor(out=h_new, in0=h_new, in1=log, op=ALU.mult)
            hcols = slice(head * DH, (head + 1) * DH)
            nc.sync.dma_start(out=batch_tiles(out_h)[:, rows, hcols], in_=h_new)

        for r in range(TPH):
            sum_zo(r)
            squash(r)
        transpose_zo(0)
        sum_if(0)
        for u in range(STEPS + 1):
            head, t, back = u // BT, u % BT, u - 1
            if u == EARLY_STEP:
                for done in range(EARLY_HEADS):
                    log_of_n(done)
            if u < STEPS:
                shift_f(u)
            if back >= 0:
                keep_states(back)
            if u < STEPS:
                difference(u)
            take_weights(17 + QUANT_LAG + 3 * u)
            if back >= 0:
                input_term(back)
                new_n(back)
            if u < STEPS:
                stabilise(u)
                exponentials(u)
            if back >= 0:
                new_c(back)
            if u + 1 < STEPS:
                sum_if(u + 1)
            if t == 1 and head + 1 < NH:
                for j in range(TPH):
                    sum_zo((head + 1) * TPH + j)
                    squash((head + 1) * TPH + j)
            if back >= 0:
                open_output(back)
                if t == 0:
                    store_states(head - 1)
                    if head < NH:
                        transpose_zo(head)
        for head in range(EARLY_HEADS):
            finish_h(head)
        for head in range(EARLY_HEADS, NH - 1):
            log_of_n(head)
        for t in range(BT):
            log_of_n(NH - 1, slice(t, t + 1))
        for head in range(EARLY_HEADS, NH - 1):
            finish_h(head)
        for t in range(BT):
            finish_h(NH - 1, slice(t, t + 1))
